import numpy as np
import ml_dtypes


def mxq(x, axis, fmt="e4m3"):
    dtype, down = {"e4m3": (ml_dtypes.float8_e4m3fn, 7), "e5m2": (ml_dtypes.float8_e5m2, 14)}[fmt]
    v = np.moveaxis(np.asarray(x, np.float32).astype(ml_dtypes.bfloat16).astype(np.float64), axis, -1)
    blocks = v.reshape(v.shape[:-1] + (-1, 32))
    amax = np.abs(blocks).max(-1, keepdims=True)
    byte = np.maximum(np.where(amax > 0, np.frexp(amax)[1] - 1 + 127, 0) - down, 1)
    scale = np.exp2(byte - 127.0)
    codes = (blocks / scale).astype(np.float32).astype(dtype).astype(np.float64)
    return np.moveaxis((codes * scale).reshape(v.shape), -1, axis)


WIDE = False


def mx_kscale(k):
    if not WIDE:
        return np.ones(k)
    levels = np.array([10, -10, 5, -5, 0])
    a = np.random.permutation(np.resize(levels, k // 512 * 4)).reshape(k // 512, 4)
    idx = np.arange(k)
    return np.exp2(a[idx // 512, idx % 128 // 32])


BF16 = ml_dtypes.bfloat16


def bf(x):
    return np.asarray(x, np.float32).astype(BF16)


def f64(x):
    return np.asarray(x).astype(np.float64)


B, C, H, W, T, HID = 128, 1024, 7, 7, 20, 512
S = H * W


def softmax_pos(h):
    e = np.exp(h - h.max(axis=1, keepdims=True))
    return e / e.sum(axis=1, keepdims=True)


def setup_inputs():
    s = mx_kscale(C)
    return {"v_i": bf(np.random.standard_normal((B, C, H, W)) * s[None, :, None, None]),
            "v_q": bf(np.random.standard_normal((B, T, HID))),
            "l1_w": bf(np.random.standard_normal((HID, C)) / np.sqrt(C) / s[None, :]),
            "l1_b": bf(np.random.standard_normal(HID) * 0.1),
            "w_vi0": bf(np.random.standard_normal((HID, HID)) * 1.5 / np.sqrt(HID)),
            "w_u0": bf(np.random.standard_normal((HID, HID)) * 2.0 / np.sqrt(HID)),
            "b_u0": bf(np.random.standard_normal(HID) * 0.5)}


def reference(v_i, v_q, l1_w, l1_b, w_vi0, w_u0, b_u0):
    x = f64(v_i).reshape(B, C, S).transpose(0, 2, 1)
    vi = np.tanh((mxq(x, 2, "e4m3") @ mxq(f64(l1_w).T, 0, "e4m3")) + f64(l1_b))
    u = f64(v_q).mean(axis=1)
    v_i_t = mxq(vi, 2, "e4m3") @ mxq(f64(w_vi0).T, 0, "e4m3")
    v_q_t = (mxq(u, 1, "e4m3") @ mxq(f64(w_u0).T, 0, "e4m3")) + f64(b_u0)
    h_a = np.tanh(v_i_t + v_q_t[:, None, :])
    p_i = softmax_pos(h_a)
    return u + (p_i * vi).sum(axis=1)

@@ -1,0 +1,287 @@
+from contextlib import ExitStack
+
+import concourse.mybir as mybir
+from concourse.masks import make_identity
+
+F32 = mybir.dt.float32
+BF16 = mybir.dt.bfloat16
+U32 = mybir.dt.uint32
+U8 = mybir.dt.uint8
+I32 = mybir.dt.int32
+FP8X4 = mybir.dt.float8_e4m3fn_x4
+FUNC = mybir.ActivationFunctionType
+ALU = mybir.AluOpType
+AXIS = mybir.AxisListType
+
+B, C, S, T, HID = 128, 1024, 49, 20, 512
+P = 128
+NCH = 4
+NB = 10
+NCOL = 512
+FLOPS = 2 * B * S * C * HID + 2 * B * S * HID * HID + 2 * B * HID * HID
+
+ACC_CHUNKS = 4
+MANUAL = False
+
+
+def tile_attentionmechanism_pa_t_kernel(tc, v_i, v_q, l1_w, l1_b, w_vi0, w_u0, b_u0, out):
+    nc = tc.nc
+    blocks = [(first, min(NB, B - first)) for first in range(0, B, NB)]
+    nblk = len(blocks)
+
+    with ExitStack() as ctx:
+        keep = ctx.enter_context(tc.tile_pool(name="keep", bufs=1))
+        rawp = ctx.enter_context(tc.tile_pool(name="rawp", bufs=3))
+        vip = ctx.enter_context(tc.tile_pool(name="vip", bufs=4))
+        hp = ctx.enter_context(tc.tile_pool(name="hp", bufs=3))
+        ps1 = ctx.enter_context(tc.psum_pool(name="ps1", bufs=4))
+        ps2 = ctx.enter_context(tc.psum_pool(name="ps2", bufs=4))
+        if MANUAL:
+            ctx.enter_context(tc.manual_schedule())
+
+        xg = [keep.tile([P, 2, NCOL, 4], BF16, align_bytes=64, name="xg%d" % i) for i in range(2)]
+        xq = [keep.tile([P, 2, NCOL], U32, align_bytes=64, name="xq%d" % i) for i in range(2)]
+        xs = [keep.tile([P, 2, NCOL], U8, align_bytes=64, name="xs%d" % i) for i in range(2)]
+        vg = [keep.tile([P, NCOL, 4], BF16, align_bytes=64, name="vg%d" % i) for i in range(2)]
+        vc = [keep.tile([P, NCOL], U32, align_bytes=64, name="vc%d" % i) for i in range(2)]
+        vs = [keep.tile([P, NCOL], U8, align_bytes=64, name="vs%d" % i) for i in range(2)]
+        for i in range(2):
+            nc.vector.memset(xg[i][:].rearrange("p g c t -> p (g c t)").bitcast(I32), 0)
+            nc.vector.memset(vg[i][:].rearrange("p c t -> p (c t)").bitcast(I32), 0)
+
+        raws = {}
+
+        def load(i):
+            b0, nb = blocks[i]
+            raw = [rawp.tile([P, NB, 4 * S], BF16, name="raw%d" % g) for g in range(2)]
+            for g in range(2):
+                nc.sync.dma_start(
+                    out=raw[g][:, :nb, :],
+                    in_=v_i[b0 : b0 + nb, g * 512 : (g + 1) * 512].rearrange("b (p t) h w -> p b (t h w)", t=4),
+                )
+            raws[i] = raw
+
+        load(0)
+        w1raw = keep.tile([P, NCH, C], BF16, name="w1raw")
+        nc.sync.dma_start(out=w1raw[:], in_=l1_w.rearrange("(j m) k -> j m k", m=NCH))
+        l1b_raw = keep.tile([P, NCH], BF16, name="l1b_raw")
+        nc.scalar.dma_start(out=l1b_raw[:], in_=l1_b.rearrange("(j m) -> j m", m=NCH))
+        bu_raw = keep.tile([P, NCH], BF16, name="bu_raw")
+        nc.scalar.dma_start(out=bu_raw[:], in_=b_u0.rearrange("(j m) -> j m", m=NCH))
+        vqr = keep.tile([P, T, HID], BF16, name="vqr")
+        for c in range(4):
+            nc.scalar.dma_start(out=vqr[:, 5 * c : 5 * c + 5, :], in_=v_q[:, 5 * c : 5 * c + 5, :])
+        w3raw = keep.tile([P, NCH, HID], BF16, name="w3raw")
+        nc.scalar.dma_start(out=w3raw[:], in_=w_u0.rearrange("(j m) k -> j m k", m=NCH))
+        w2raw = keep.tile([P, NCH, HID], BF16, name="w2raw")
+        nc.scalar.dma_start(out=w2raw[:], in_=w_vi0.rearrange("(j m) k -> j m k", m=NCH))
+        load(1)
+        load(2)
+
+        ident32 = keep.tile([P, P], F32, name="ident32")
+        make_identity(nc, ident32[:])
+        identb = keep.tile([P, P], BF16, name="identb")
+        make_identity(nc, identb[:])
+
+        l1b = keep.tile([P, NCH], F32, name="l1b")
+        nc.vector.tensor_copy(out=l1b[:], in_=l1b_raw[:])
+        bu = keep.tile([P, NCH], F32, name="bu")
+        nc.vector.tensor_copy(out=bu[:], in_=bu_raw[:])
+
+        def prep_weight(raw, passes, nm):
+            grp = keep.tile([P, passes, NCH, P, 4], BF16, align_bytes=64, name=nm + "g")
+            codes = keep.tile([P, passes, NCH * P], U32, align_bytes=64, name=nm + "q")
+            scales = keep.tile([P, passes, NCH * P], U8, align_bytes=64, name=nm + "s")
+            for g in range(passes):
+                for mh in range(2):
+                    pt = ps1.tile([P, 2, 2, P], F32, name="pt", tag="ps1")
+                    for mm in range(2):
+                        words = raw[:, 2 * mh + mm, :].bitcast(F32).rearrange("p (g q u) -> p g u q", g=passes, u=2)
+                        for u in range(2):
+                            nc.tensor.transpose(pt[:, mm, u, :], words[:, g, u, :], ident32[:])
+                    nc.scalar.copy(
+                        out=grp[:, g, 2 * mh : 2 * mh + 2, :, :].bitcast(F32),
+                        in_=pt[:].rearrange("p a u j -> p a j u"),
+                    )
+            return grp, codes, scales
+
+        def quant_weight(grp, codes, scales, passes):
+            for g in range(passes):
+                nc.vector.quantize_mx(
+                    out=codes[:, g, :].bitcast(FP8X4),
+                    scales=scales[:, g, :],
+                    in_=grp[:, g].rearrange("p m j t -> p (m j t)"),
+                )
+
+        def rx(i):
+            b0, nb = blocks[i]
+            raw = raws[i]
+            for g in range(2):
+                nc.vector.tensor_copy(
+                    out=xg[i % 2][:, g, : nb * S, :].rearrange("p (b s) t -> p b s t", s=S),
+                    in_=raw[g][:, :nb, :].rearrange("p b (t s) -> p b s t", t=4),
+                )
+
+        def qx(i):
+            nc.vector.quantize_mx(
+                out=xq[i % 2][:].rearrange("p g c -> p (g c)").bitcast(FP8X4),
+                scales=xs[i % 2][:].rearrange("p g c -> p (g c)"),
+                in_=xg[i % 2][:].rearrange("p g c t -> p (g c t)"),
+            )
+
+        vis = {}
+        hs = {}
+
+        def mm1(i):
+            b0, nb = blocks[i]
+            cols = nb * S
+            vi = vip.tile([P, NCH, NB * S], F32, name="vi")
+            vis[i] = vi
+            for m in range(NCH):
+                ps = ps1.tile([P, NCOL], F32, name="ps", tag="ps1")
+                for g in range(2):
+                    nc.tensor.matmul_mx(
+                        out=ps[:],
+                        lhsT=w1q[:, g, m * P : (m + 1) * P].bitcast(FP8X4),
+                        lhsT_scale=w1s[:, g, m * P : (m + 1) * P],
+                        rhs=xq[i % 2][:, g, :].bitcast(FP8X4),
+                        rhs_scale=xs[i % 2][:, g, :],
+                        start=(g == 0),
+                        stop=(g == 1),
+                    )
+                nc.scalar.activation(out=vi[:, m, :cols], in_=ps[:, :cols], func=FUNC.Tanh, bias=l1b[:, m : m + 1])
+
+        def vgroup(i):
+            b0, nb = blocks[i]
+            cols = nb * S
+            nc.vector.tensor_copy(out=vg[i % 2][:, :cols, :], in_=vis[i][:, :, :cols].rearrange("p m c -> p c m"))
+
+        def qv(i):
+            nc.vector.quantize_mx(
+                out=vc[i % 2][:].bitcast(FP8X4),
+                scales=vs[i % 2][:],
+                in_=vg[i % 2][:].rearrange("p c t -> p (c t)"),
+            )
+
+        def mm2(i):
+            b0, nb = blocks[i]
+            cols = nb * S
+            h = hp.tile([P, NCH, NB * S], F32, name="h")
+            hs[i] = h
+            for m in range(NCH):
+                ps = ps2.tile([P, NCOL], F32, name="pz", tag="ps2")
+                nc.tensor.matmul_mx(
+                    out=ps[:],
+                    lhsT=w2q[:, 0, m * P : (m + 1) * P].bitcast(FP8X4),
+                    lhsT_scale=w2s[:, 0, m * P : (m + 1) * P],
+                    rhs=vc[i % 2][:].bitcast(FP8X4),
+                    rhs_scale=vs[i % 2][:],
+                    start=True,
+                    stop=True,
+                )
+                for b in range(nb):
+                    nc.scalar.activation(
+                        out=h[:, m, b * S : (b + 1) * S],
+                        in_=ps[:, b * S : (b + 1) * S],
+                        func=FUNC.Tanh,
+                        bias=vqb[:, m, b0 + b : b0 + b + 1],
+                    )
+            for m in range(ACC_CHUNKS):
+                for b in range(nb):
+                    nc.scalar.activation(
+                        out=h[:, m, b * S : (b + 1) * S],
+                        in_=h[:, m, b * S : (b + 1) * S],
+                        func=FUNC.Exp,
+                        accum_out=den[:, m, b0 + b : b0 + b + 1],
+                    )
+            if ACC_CHUNKS < NCH:
+                nc.scalar.activation(out=h[:, ACC_CHUNKS:, :cols], in_=h[:, ACC_CHUNKS:, :cols], func=FUNC.Exp)
+
+        def wsum(i):
+            b0, nb = blocks[i]
+            cols = nb * S
+            h = hs[i]
+            vi = vis[i]
+            if ACC_CHUNKS < NCH:
+                nc.vector.tensor_reduce(
+                    out=den[:, ACC_CHUNKS:, b0 : b0 + nb],
+                    in_=h[:, ACC_CHUNKS:, :cols].rearrange("p m (b s) -> p m b s", s=S),
+                    axis=AXIS.X,
+                    op=ALU.add,
+                )
+            nc.vector.tensor_tensor(out=h[:, :, :cols], in0=h[:, :, :cols], in1=vi[:, :, :cols], op=ALU.mult)
+            nc.vector.tensor_reduce(
+                out=num[:, :, b0 : b0 + nb],
+                in_=h[:, :, :cols].rearrange("p m (b s) -> p m b s", s=S),
+                axis=AXIS.X,
+                op=ALU.add,
+            )
+
+        num = keep.tile([P, NCH, B], F32, name="num")
+        den = keep.tile([P, NCH, B], F32, name="den")
+
+        rx(0)
+        w1g, w1q, w1s = prep_weight(w1raw, 2, "w1")
+        qx(0)
+        quant_weight(w1g, w1q, w1s, 2)
+        mm1(0)
+
+        pus = [ps2.tile([P, NCOL], F32, name="pu%d" % m, tag="ps2") for m in range(NCH)]
+        for t in range(T):
+            cols4 = vqr[:, t, :].rearrange("p (j m) -> p m j", m=NCH)
+            for m in range(NCH):
+                nc.tensor.matmul(pus[m][:, :P], lhsT=cols4[:, m, :], rhs=identb[:], start=(t == 0), stop=(t == T - 1))
+        uT = keep.tile([P, NCH, B], F32, name="uT")
+        for m in range(NCH):
+            nc.scalar.mul(out=uT[:, m, :], in_=pus[m][:, :P], mul=1.0 / T)
+        ug = keep.tile([P, B, 4], BF16, align_bytes=64, name="ug")
+        nc.vector.tensor_copy(out=ug[:], in_=uT[:].rearrange("p m b -> p b m"))
+        uq = keep.tile([P, B], U32, align_bytes=64, name="uq")
+        us = keep.tile([P, B], U8, align_bytes=64, name="us")
+        w3g, w3q, w3s = prep_weight(w3raw, 1, "w3")
+        nc.vector.quantize_mx(out=uq[:].bitcast(FP8X4), scales=us[:], in_=ug[:].rearrange("p b t -> p (b t)"))
+        quant_weight(w3g, w3q, w3s, 1)
+        w2g, w2q, w2s = prep_weight(w2raw, 1, "w2")
+        quant_weight(w2g, w2q, w2s, 1)
+        pv = ps2.tile([P, NCH, P], F32, name="pv", tag="ps2")
+        vqb = keep.tile([P, NCH, B], F32, name="vqb")
+        for m in range(NCH):
+            nc.tensor.matmul_mx(
+                out=pv[:, m, :],
+                lhsT=w3q[:, 0, m * P : (m + 1) * P].bitcast(FP8X4),
+                lhsT_scale=w3s[:, 0, m * P : (m + 1) * P],
+                rhs=uq[:].bitcast(FP8X4),
+                rhs_scale=us[:],
+                start=True,
+                stop=True,
+            )
+            nc.scalar.activation(out=vqb[:, m, :], in_=pv[:, m, :], func=FUNC.Identity, bias=bu[:, m : m + 1])
+
+        for k in range(nblk + 1):
+            if k + 3 < nblk:
+                load(k + 3)
+            if k + 1 < nblk:
+                rx(k + 1)
+            if k < nblk:
+                vgroup(k)
+            if k + 1 < nblk:
+                qx(k + 1)
+            if k < nblk:
+                qv(k)
+            if k + 1 < nblk:
+                mm1(k + 1)
+            if k < nblk:
+                mm2(k)
+            if k >= 1:
+                wsum(k - 1)
+
+        rden = keep.tile([P, NCH, B], F32, name="rden")
+        nc.vector.reciprocal(out=rden[:], in_=den[:])
+        nc.vector.tensor_tensor(out=num[:], in0=num[:], in1=rden[:], op=ALU.mult)
+        nc.vector.tensor_tensor(out=num[:], in0=num[:], in1=uT[:], op=ALU.add)
+        po = ps1.tile([P, NCH, P], F32, name="po", tag="ps1")
+        for m in range(NCH):
+            nc.tensor.transpose(po[:, m, :], num[:, m, :], ident32[:])
+        osb = keep.tile([P, P, NCH], F32, name="osb")
+        nc.vector.tensor_copy(out=osb[:], in_=po[:].rearrange("b m j -> b j m"))
+        nc.sync.dma_start(out=out[:, :], in_=osb[:].rearrange("b j m -> b (j m)"))

@@ -16,24 +16,34 @@ AXIS = mybir.AxisListType
 B, C, S, T, HID = 128, 1024, 49, 20, 512
 P = 128
 NCH = 4
-NB = 10
 NCOL = 512
+HPAD = 496
 FLOPS = 2 * B * S * C * HID + 2 * B * S * HID * HID + 2 * B * HID * HID
 
-ACC_CHUNKS = 4
-MANUAL = False
+SIZES = [10] * 12 + [8]
+ACC_CHUNKS = 1
+POOL_CHUNKS = 4
+RUN4 = False
+RX_ACT = {}
+MANUAL = True
+RAW_BUFS = 3
+VI_BUFS = 5
+H_BUFS = 3
+PR_BUFS = 3
 
 
 def tile_attentionmechanism_pa_t_kernel(tc, v_i, v_q, l1_w, l1_b, w_vi0, w_u0, b_u0, out):
     nc = tc.nc
-    blocks = [(first, min(NB, B - first)) for first in range(0, B, NB)]
-    nblk = len(blocks)
+    nblk = len(SIZES)
+    blocks = [(sum(SIZES[:i]), SIZES[i]) for i in range(nblk)]
+    nbmax = max(SIZES)
 
     with ExitStack() as ctx:
         keep = ctx.enter_context(tc.tile_pool(name="keep", bufs=1))
-        rawp = ctx.enter_context(tc.tile_pool(name="rawp", bufs=3))
-        vip = ctx.enter_context(tc.tile_pool(name="vip", bufs=4))
-        hp = ctx.enter_context(tc.tile_pool(name="hp", bufs=3))
+        rawp = ctx.enter_context(tc.tile_pool(name="rawp", bufs=RAW_BUFS))
+        vip = ctx.enter_context(tc.tile_pool(name="vip", bufs=VI_BUFS))
+        hp = ctx.enter_context(tc.tile_pool(name="hp", bufs=H_BUFS))
+        prp = ctx.enter_context(tc.tile_pool(name="prp", bufs=PR_BUFS))
         ps1 = ctx.enter_context(tc.psum_pool(name="ps1", bufs=4))
         ps2 = ctx.enter_context(tc.psum_pool(name="ps2", bufs=4))
         if MANUAL:
@@ -49,11 +59,49 @@ def tile_attentionmechanism_pa_t_kernel(tc, v_i, v_q, l1_w, l1_b, w_vi0, w_u0, b
             nc.vector.memset(xg[i][:].rearrange("p g c t -> p (g c t)").bitcast(I32), 0)
             nc.vector.memset(vg[i][:].rearrange("p c t -> p (c t)").bitcast(I32), 0)
 
+        ident32 = keep.tile([P, P], F32, name="ident32")
+        make_identity(nc, ident32[:])
+        identb = keep.tile([P, P], BF16, name="identb")
+        make_identity(nc, identb[:])
+
+        wraw = {
+            "w1": keep.tile([P, NCH, C], BF16, name="w1raw"),
+            "w2": keep.tile([P, NCH, HID], BF16, name="w2raw"),
+            "w3": keep.tile([P, NCH, HID], BF16, name="w3raw"),
+        }
+        wsrc = {"w1": l1_w, "w2": w_vi0, "w3": w_u0}
+        wpass = {"w1": 2, "w2": 1, "w3": 1}
+        wgrp = {}
+        wq_ = {}
+        ws_ = {}
+        for nm in ("w1", "w2", "w3"):
+            wgrp[nm] = keep.tile([P, wpass[nm], NCH, P, 4], BF16, align_bytes=64, name=nm + "g")
+            wq_[nm] = keep.tile([P, wpass[nm], NCH * P], U32, align_bytes=64, name=nm + "q")
+            ws_[nm] = keep.tile([P, wpass[nm], NCH * P], U8, align_bytes=64, name=nm + "s")
+        vqr = keep.tile([P, T, HID], BF16, name="vqr")
+        l1b_raw = keep.tile([P, NCH], BF16, name="l1b_raw")
+        bu_raw = keep.tile([P, NCH], BF16, name="bu_raw")
+        l1b = keep.tile([P, NCH], F32, name="l1b")
+        bu = keep.tile([P, NCH], F32, name="bu")
+        u32 = keep.tile([P, NCH, P], F32, name="u32")
+        ug = keep.tile([P, B, 4], BF16, align_bytes=64, name="ug")
+        uq = keep.tile([P, B], U32, align_bytes=64, name="uq")
+        us = keep.tile([P, B], U8, align_bytes=64, name="us")
+        vqb = keep.tile([P, NCH, B], F32, name="vqb")
+        num = keep.tile([P, NCH, B], F32, name="num")
+        den = keep.tile([P, NCH, B], F32, name="den")
+        rden = keep.tile([P, NCH, B], F32, name="rden")
+        osb = keep.tile([P, P, NCH], F32, name="osb")
+
         raws = {}
+        vis = {}
+        hs = {}
+        pst = {}
+        prs = {}
 
         def load(i):
             b0, nb = blocks[i]
-            raw = [rawp.tile([P, NB, 4 * S], BF16, name="raw%d" % g) for g in range(2)]
+            raw = [rawp.tile([P, nbmax, 4 * S], BF16, name="raw%d" % g) for g in range(2)]
             for g in range(2):
                 nc.sync.dma_start(
                     out=raw[g][:, :nb, :],
@@ -61,66 +109,56 @@ def tile_attentionmechanism_pa_t_kernel(tc, v_i, v_q, l1_w, l1_b, w_vi0, w_u0, b
                 )
             raws[i] = raw
 
-        load(0)
-        w1raw = keep.tile([P, NCH, C], BF16, name="w1raw")
-        nc.sync.dma_start(out=w1raw[:], in_=l1_w.rearrange("(j m) k -> j m k", m=NCH))
-        l1b_raw = keep.tile([P, NCH], BF16, name="l1b_raw")
-        nc.scalar.dma_start(out=l1b_raw[:], in_=l1_b.rearrange("(j m) -> j m", m=NCH))
-        bu_raw = keep.tile([P, NCH], BF16, name="bu_raw")
-        nc.scalar.dma_start(out=bu_raw[:], in_=b_u0.rearrange("(j m) -> j m", m=NCH))
-        vqr = keep.tile([P, T, HID], BF16, name="vqr")
-        for c in range(4):
-            nc.scalar.dma_start(out=vqr[:, 5 * c : 5 * c + 5, :], in_=v_q[:, 5 * c : 5 * c + 5, :])
-        w3raw = keep.tile([P, NCH, HID], BF16, name="w3raw")
-        nc.scalar.dma_start(out=w3raw[:], in_=w_u0.rearrange("(j m) k -> j m k", m=NCH))
-        w2raw = keep.tile([P, NCH, HID], BF16, name="w2raw")
-        nc.scalar.dma_start(out=w2raw[:], in_=w_vi0.rearrange("(j m) k -> j m k", m=NCH))
-        load(1)
-        load(2)
+        def loadw(nm):
+            nc.sync.dma_start(out=wraw[nm][:], in_=wsrc[nm].rearrange("(j m) k -> j m k", m=NCH))
 
-        ident32 = keep.tile([P, P], F32, name="ident32")
-        make_identity(nc, ident32[:])
-        identb = keep.tile([P, P], BF16, name="identb")
-        make_identity(nc, identb[:])
+        def loadvq():
+            for c in range(4):
+                nc.sync.dma_start(out=vqr[:, 5 * c : 5 * c + 5, :], in_=v_q[:, 5 * c : 5 * c + 5, :])
 
-        l1b = keep.tile([P, NCH], F32, name="l1b")
-        nc.vector.tensor_copy(out=l1b[:], in_=l1b_raw[:])
-        bu = keep.tile([P, NCH], F32, name="bu")
-        nc.vector.tensor_copy(out=bu[:], in_=bu_raw[:])
+        def loadb():
+            nc.scalar.dma_start(out=l1b_raw[:], in_=l1_b.rearrange("(j m) -> j m", m=NCH))
+            nc.scalar.dma_start(out=bu_raw[:], in_=b_u0.rearrange("(j m) -> j m", m=NCH))
 
-        def prep_weight(raw, passes, nm):
-            grp = keep.tile([P, passes, NCH, P, 4], BF16, align_bytes=64, name=nm + "g")
-            codes = keep.tile([P, passes, NCH * P], U32, align_bytes=64, name=nm + "q")
-            scales = keep.tile([P, passes, NCH * P], U8, align_bytes=64, name=nm + "s")
-            for g in range(passes):
-                for mh in range(2):
-                    pt = ps1.tile([P, 2, 2, P], F32, name="pt", tag="ps1")
-                    for mm in range(2):
-                        words = raw[:, 2 * mh + mm, :].bitcast(F32).rearrange("p (g q u) -> p g u q", g=passes, u=2)
-                        for u in range(2):
-                            nc.tensor.transpose(pt[:, mm, u, :], words[:, g, u, :], ident32[:])
-                    nc.scalar.copy(
-                        out=grp[:, g, 2 * mh : 2 * mh + 2, :, :].bitcast(F32),
-                        in_=pt[:].rearrange("p a u j -> p a j u"),
-                    )
-            return grp, codes, scales
+        def castb():
+            nc.vector.tensor_copy(out=l1b[:], in_=l1b_raw[:])
+            nc.vector.tensor_copy(out=bu[:], in_=bu_raw[:])
 
-        def quant_weight(grp, codes, scales, passes):
-            for g in range(passes):
-                nc.vector.quantize_mx(
-                    out=codes[:, g, :].bitcast(FP8X4),
-                    scales=scales[:, g, :],
-                    in_=grp[:, g].rearrange("p m j t -> p (m j t)"),
+        def wt(nm, g):
+            for mh in range(2):
+                pt = ps1.tile([P, 2, 2, P], F32, name="pt", tag="ps1")
+                for mm in range(2):
+                    words = wraw[nm][:, 2 * mh + mm, :].bitcast(F32).rearrange("p (g q u) -> p g u q", g=wpass[nm], u=2)
+                    for u in range(2):
+                        nc.tensor.transpose(pt[:, mm, u, :], words[:, g, u, :], ident32[:])
+                nc.scalar.copy(
+                    out=wgrp[nm][:, g, 2 * mh : 2 * mh + 2, :, :].bitcast(F32),
+                    in_=pt[:].rearrange("p a u j -> p a j u"),
                 )
+
+        def wq(nm, g):
+            nc.vector.quantize_mx(
+                out=wq_[nm][:, g, :].bitcast(FP8X4),
+                scales=ws_[nm][:, g, :],
+                in_=wgrp[nm][:, g].rearrange("p m j t -> p (m j t)"),
+            )
 
         def rx(i):
             b0, nb = blocks[i]
             raw = raws[i]
             for g in range(2):
-                nc.vector.tensor_copy(
-                    out=xg[i % 2][:, g, : nb * S, :].rearrange("p (b s) t -> p b s t", s=S),
-                    in_=raw[g][:, :nb, :].rearrange("p b (t s) -> p b s t", t=4),
-                )
+                dst = xg[i % 2][:, g, : nb * S, :].rearrange("p (b s) t -> p b s t", s=S)
+                src = raw[g][:, :nb, :].rearrange("p b (t s) -> p b t s", t=4)
+                if RX_ACT.get(i, 0) > g:
+                    nc.scalar.copy(out=dst, in_=src.rearrange("p b t s -> p b s t"))
+                elif RUN4:
+                    nc.vector.tensor_copy(
+                        out=dst[:, :, :48, :].rearrange("p b (c i) t -> p b c t i", i=4),
+                        in_=src[:, :, :, :48].rearrange("p b t (c i) -> p b c t i", i=4),
+                    )
+                    nc.vector.tensor_copy(out=dst[:, :, 48, :], in_=src[:, :, :, 48])
+                else:
+                    nc.vector.tensor_copy(out=dst, in_=src.rearrange("p b t s -> p b s t"))
 
         def qx(i):
             nc.vector.quantize_mx(
@@ -129,21 +167,18 @@ def tile_attentionmechanism_pa_t_kernel(tc, v_i, v_q, l1_w, l1_b, w_vi0, w_u0, b
                 in_=xg[i % 2][:].rearrange("p g c t -> p (g c t)"),
             )
 
-        vis = {}
-        hs = {}
-
         def mm1(i):
             b0, nb = blocks[i]
             cols = nb * S
-            vi = vip.tile([P, NCH, NB * S], F32, name="vi")
+            vi = vip.tile([P, NCH, nbmax * S], F32, name="vi")
             vis[i] = vi
             for m in range(NCH):
                 ps = ps1.tile([P, NCOL], F32, name="ps", tag="ps1")
                 for g in range(2):
                     nc.tensor.matmul_mx(
                         out=ps[:],
-                        lhsT=w1q[:, g, m * P : (m + 1) * P].bitcast(FP8X4),
-                        lhsT_scale=w1s[:, g, m * P : (m + 1) * P],
+                        lhsT=wq_["w1"][:, g, m * P : (m + 1) * P].bitcast(FP8X4),
+                        lhsT_scale=ws_["w1"][:, g, m * P : (m + 1) * P],
                         rhs=xq[i % 2][:, g, :].bitcast(FP8X4),
                         rhs_scale=xs[i % 2][:, g, :],
                         start=(g == 0),
@@ -151,7 +186,7 @@ def tile_attentionmechanism_pa_t_kernel(tc, v_i, v_q, l1_w, l1_b, w_vi0, w_u0, b
                     )
                 nc.scalar.activation(out=vi[:, m, :cols], in_=ps[:, :cols], func=FUNC.Tanh, bias=l1b[:, m : m + 1])
 
-        def vgroup(i):
+        def v(i):
             b0, nb = blocks[i]
             cols = nb * S
             nc.vector.tensor_copy(out=vg[i % 2][:, :cols, :], in_=vis[i][:, :, :cols].rearrange("p m c -> p c m"))
@@ -163,125 +198,180 @@ def tile_attentionmechanism_pa_t_kernel(tc, v_i, v_q, l1_w, l1_b, w_vi0, w_u0, b
                 in_=vg[i % 2][:].rearrange("p c t -> p (c t)"),
             )
 
+        def uc(c):
+            if c == 0:
+                pst["pu"] = ps2.tile([P, HID], F32, name="pu", tag="ps2")
+            for t in range(5 * c, 5 * c + 5):
+                nc.tensor.matmul(pst["pu"][:], lhsT=identb[:], rhs=vqr[:, t, :], start=(t == 0), stop=(t == T - 1))
+
+        def usc():
+            nc.scalar.activation(
+                out=u32[:], in_=pst["pu"][:].rearrange("b (j m) -> b m j", m=NCH), func=FUNC.Copy, scale=1.0 / T
+            )
+            pst["put"] = ps2.tile([P, NCH, P], F32, name="put", tag="ps2")
+            for m in range(NCH):
+                nc.tensor.transpose(pst["put"][:, m, :], u32[:, m, :], ident32[:])
+
+        def ugr():
+            nc.vector.tensor_copy(out=ug[:], in_=pst["put"][:].rearrange("j m b -> j b m"))
+
+        def uqu():
+            nc.vector.quantize_mx(out=uq[:].bitcast(FP8X4), scales=us[:], in_=ug[:].rearrange("p b t -> p (b t)"))
+
+        def mm3():
+            pv = ps2.tile([P, NCH, P], F32, name="pv", tag="ps2")
+            for m in range(NCH):
+                nc.tensor.matmul_mx(
+                    out=pv[:, m, :],
+                    lhsT=wq_["w3"][:, 0, m * P : (m + 1) * P].bitcast(FP8X4),
+                    lhsT_scale=ws_["w3"][:, 0, m * P : (m + 1) * P],
+                    rhs=uq[:].bitcast(FP8X4),
+                    rhs_scale=us[:],
+                    start=True,
+                    stop=True,
+                )
+            for m in range(NCH):
+                nc.scalar.activation(out=vqb[:, m, :], in_=pv[:, m, :], func=FUNC.Identity, bias=bu[:, m : m + 1])
+
         def mm2(i):
             b0, nb = blocks[i]
             cols = nb * S
-            h = hp.tile([P, NCH, NB * S], F32, name="h")
+            h = hp.tile([P, NCH, HPAD], F32, name="h")
             hs[i] = h
+            banks = []
             for m in range(NCH):
                 ps = ps2.tile([P, NCOL], F32, name="pz", tag="ps2")
+                banks.append(ps)
                 nc.tensor.matmul_mx(
                     out=ps[:],
-                    lhsT=w2q[:, 0, m * P : (m + 1) * P].bitcast(FP8X4),
-                    lhsT_scale=w2s[:, 0, m * P : (m + 1) * P],
+                    lhsT=wq_["w2"][:, 0, m * P : (m + 1) * P].bitcast(FP8X4),
+                    lhsT_scale=ws_["w2"][:, 0, m * P : (m + 1) * P],
                     rhs=vc[i % 2][:].bitcast(FP8X4),
                     rhs_scale=vs[i % 2][:],
                     start=True,
                     stop=True,
                 )
+            for m in range(NCH):
                 for b in range(nb):
                     nc.scalar.activation(
                         out=h[:, m, b * S : (b + 1) * S],
-                        in_=ps[:, b * S : (b + 1) * S],
+                        in_=banks[m][:, b * S : (b + 1) * S],
                         func=FUNC.Tanh,
                         bias=vqb[:, m, b0 + b : b0 + b + 1],
                     )
-            for m in range(ACC_CHUNKS):
-                for b in range(nb):
-                    nc.scalar.activation(
-                        out=h[:, m, b * S : (b + 1) * S],
-                        in_=h[:, m, b * S : (b + 1) * S],
-                        func=FUNC.Exp,
-                        accum_out=den[:, m, b0 + b : b0 + b + 1],
-                    )
-            if ACC_CHUNKS < NCH:
-                nc.scalar.activation(out=h[:, ACC_CHUNKS:, :cols], in_=h[:, ACC_CHUNKS:, :cols], func=FUNC.Exp)
+                if m < ACC_CHUNKS:
+                    for b in range(nb):
+                        nc.scalar.activation(
+                            out=h[:, m, b * S : (b + 1) * S],
+                            in_=h[:, m, b * S : (b + 1) * S],
+                            func=FUNC.Exp,
+                            accum_out=den[:, m, b0 + b : b0 + b + 1],
+                        )
+                else:
+                    nc.scalar.activation(out=h[:, m, :cols], in_=h[:, m, :cols], func=FUNC.Exp)
 
-        def wsum(i):
+        def prod(i):
             b0, nb = blocks[i]
             cols = nb * S
             h = hs[i]
             vi = vis[i]
+            pr = prp.tile([P, NCH, HPAD], F32, name="pr")
+            prs[i] = pr
+            nv = NCH if i == nblk - 1 else NCH - POOL_CHUNKS
+            for m in range(nv, NCH):
+                nc.gpsimd.tensor_tensor(out=pr[:, m, :cols], in0=h[:, m, :cols], in1=vi[:, m, :cols], op=ALU.mult)
+            if nv > 0:
+                nc.vector.tensor_tensor(out=pr[:, :nv, :cols], in0=h[:, :nv, :cols], in1=vi[:, :nv, :cols], op=ALU.mult)
+
+        def sume(i):
+            b0, nb = blocks[i]
+            cols = nb * S
             if ACC_CHUNKS < NCH:
                 nc.vector.tensor_reduce(
                     out=den[:, ACC_CHUNKS:, b0 : b0 + nb],
-                    in_=h[:, ACC_CHUNKS:, :cols].rearrange("p m (b s) -> p m b s", s=S),
+                    in_=hs[i][:, ACC_CHUNKS:, :cols].rearrange("p m (b s) -> p m b s", s=S),
                     axis=AXIS.X,
                     op=ALU.add,
                 )
-            nc.vector.tensor_tensor(out=h[:, :, :cols], in0=h[:, :, :cols], in1=vi[:, :, :cols], op=ALU.mult)
+
+        def sump(i):
+            b0, nb = blocks[i]
+            cols = nb * S
             nc.vector.tensor_reduce(
                 out=num[:, :, b0 : b0 + nb],
-                in_=h[:, :, :cols].rearrange("p m (b s) -> p m b s", s=S),
+                in_=prs[i][:, :, :cols].rearrange("p m (b s) -> p m b s", s=S),
                 axis=AXIS.X,
                 op=ALU.add,
             )
 
-        num = keep.tile([P, NCH, B], F32, name="num")
-        den = keep.tile([P, NCH, B], F32, name="den")
+        def ratio(lo, hi):
+            nc.vector.reciprocal(out=rden[:, :, lo:hi], in_=den[:, :, lo:hi])
+            nc.vector.tensor_tensor(out=num[:, :, lo:hi], in0=num[:, :, lo:hi], in1=rden[:, :, lo:hi], op=ALU.mult)
 
-        rx(0)
-        w1g, w1q, w1s = prep_weight(w1raw, 2, "w1")
-        qx(0)
-        quant_weight(w1g, w1q, w1s, 2)
-        mm1(0)
-
-        pus = [ps2.tile([P, NCOL], F32, name="pu%d" % m, tag="ps2") for m in range(NCH)]
-        for t in range(T):
-            cols4 = vqr[:, t, :].rearrange("p (j m) -> p m j", m=NCH)
+        def finish():
+            po = ps1.tile([P, NCH, P], F32, name="po", tag="ps1")
             for m in range(NCH):
-                nc.tensor.matmul(pus[m][:, :P], lhsT=cols4[:, m, :], rhs=identb[:], start=(t == 0), stop=(t == T - 1))
-        uT = keep.tile([P, NCH, B], F32, name="uT")
-        for m in range(NCH):
-            nc.scalar.mul(out=uT[:, m, :], in_=pus[m][:, :P], mul=1.0 / T)
-        ug = keep.tile([P, B, 4], BF16, align_bytes=64, name="ug")
-        nc.vector.tensor_copy(out=ug[:], in_=uT[:].rearrange("p m b -> p b m"))
-        uq = keep.tile([P, B], U32, align_bytes=64, name="uq")
-        us = keep.tile([P, B], U8, align_bytes=64, name="us")
-        w3g, w3q, w3s = prep_weight(w3raw, 1, "w3")
-        nc.vector.quantize_mx(out=uq[:].bitcast(FP8X4), scales=us[:], in_=ug[:].rearrange("p b t -> p (b t)"))
-        quant_weight(w3g, w3q, w3s, 1)
-        w2g, w2q, w2s = prep_weight(w2raw, 1, "w2")
-        quant_weight(w2g, w2q, w2s, 1)
-        pv = ps2.tile([P, NCH, P], F32, name="pv", tag="ps2")
-        vqb = keep.tile([P, NCH, B], F32, name="vqb")
-        for m in range(NCH):
-            nc.tensor.matmul_mx(
-                out=pv[:, m, :],
-                lhsT=w3q[:, 0, m * P : (m + 1) * P].bitcast(FP8X4),
-                lhsT_scale=w3s[:, 0, m * P : (m + 1) * P],
-                rhs=uq[:].bitcast(FP8X4),
-                rhs_scale=us[:],
-                start=True,
-                stop=True,
+                nc.tensor.transpose(po[:, m, :], num[:, m, :], ident32[:])
+            nc.vector.tensor_tensor(
+                out=osb[:],
+                in0=po[:].rearrange("b m j -> b j m"),
+                in1=u32[:].rearrange("b m j -> b j m"),
+                op=ALU.add,
             )
-            nc.scalar.activation(out=vqb[:, m, :], in_=pv[:, m, :], func=FUNC.Identity, bias=bu[:, m : m + 1])
+            nc.sync.dma_start(out=out[:, :], in_=osb[:].rearrange("b j m -> b (j m)"))
 
-        for k in range(nblk + 1):
-            if k + 3 < nblk:
-                load(k + 3)
+        loadb()
+        loadw("w1")
+        load(0)
+        load(1)
+        loadvq()
+        loadw("w3")
+        loadw("w2")
+        load(2)
+        castb()
+        wt("w1", 0)
+        wt("w1", 1)
+        rx(0)
+        wq("w1", 0)
+        wq("w1", 1)
+        qx(0)
+        mm1(0)
+        rx(1)
+        qx(1)
+        uc(0)
+        mm1(1)
+        uc(1)
+        uc(2)
+        uc(3)
+        usc()
+        wt("w3", 0)
+        wt("w2", 0)
+        v(0)
+        qv(0)
+        ugr()
+        uqu()
+        wq("w3", 0)
+        mm3()
+        wq("w2", 0)
+        for k in range(nblk + 2):
+            if 1 <= k and k + 2 < nblk:
+                load(k + 2)
+            if k + 2 < nblk:
+                rx(k + 2)
+                qx(k + 2)
             if k + 1 < nblk:
-                rx(k + 1)
-            if k < nblk:
-                vgroup(k)
-            if k + 1 < nblk:
-                qx(k + 1)
-            if k < nblk:
-                qv(k)
-            if k + 1 < nblk:
-                mm1(k + 1)
+                v(k + 1)
+                qv(k + 1)
             if k < nblk:
                 mm2(k)
-            if k >= 1:
-                wsum(k - 1)
-
-        rden = keep.tile([P, NCH, B], F32, name="rden")
-        nc.vector.reciprocal(out=rden[:], in_=den[:])
-        nc.vector.tensor_tensor(out=num[:], in0=num[:], in1=rden[:], op=ALU.mult)
-        nc.vector.tensor_tensor(out=num[:], in0=num[:], in1=uT[:], op=ALU.add)
-        po = ps1.tile([P, NCH, P], F32, name="po", tag="ps1")
-        for m in range(NCH):
-            nc.tensor.transpose(po[:, m, :], num[:, m, :], ident32[:])
-        osb = keep.tile([P, P, NCH], F32, name="osb")
-        nc.vector.tensor_copy(out=osb[:], in_=po[:].rearrange("b m j -> b j m"))
-        nc.sync.dma_start(out=out[:, :], in_=osb[:].rearrange("b j m -> b (j m)"))
+            if k + 2 < nblk:
+                mm1(k + 2)
+            if k >= 2:
+                sump(k - 2)
+            if k == nblk:
+                ratio(0, blocks[nblk - 1][0])
+            if 1 <= k <= nblk:
+                prod(k - 1)
+                sume(k - 1)
+        ratio(blocks[nblk - 1][0], B)
+        finish()

@@ -21,15 +21,16 @@ HPAD = 496
 FLOPS = 2 * B * S * C * HID + 2 * B * S * HID * HID + 2 * B * HID * HID
 
 SIZES = [10] * 12 + [8]
-ACC_CHUNKS = 1
-POOL_CHUNKS = 4
+ACC_EARLY = 4
+ACC_LATE = 0
+B_SPLIT = 80
+POOL_CHUNKS = 0
 RUN4 = False
 RX_ACT = {}
 MANUAL = True
 RAW_BUFS = 3
 VI_BUFS = 5
 H_BUFS = 3
-PR_BUFS = 3
 
 
 def tile_attentionmechanism_pa_t_kernel(tc, v_i, v_q, l1_w, l1_b, w_vi0, w_u0, b_u0, out):
@@ -43,7 +44,6 @@ def tile_attentionmechanism_pa_t_kernel(tc, v_i, v_q, l1_w, l1_b, w_vi0, w_u0, b
         rawp = ctx.enter_context(tc.tile_pool(name="rawp", bufs=RAW_BUFS))
         vip = ctx.enter_context(tc.tile_pool(name="vip", bufs=VI_BUFS))
         hp = ctx.enter_context(tc.tile_pool(name="hp", bufs=H_BUFS))
-        prp = ctx.enter_context(tc.tile_pool(name="prp", bufs=PR_BUFS))
         ps1 = ctx.enter_context(tc.psum_pool(name="ps1", bufs=4))
         ps2 = ctx.enter_context(tc.psum_pool(name="ps2", bufs=4))
         if MANUAL:
@@ -97,7 +97,9 @@ def tile_attentionmechanism_pa_t_kernel(tc, v_i, v_q, l1_w, l1_b, w_vi0, w_u0, b
         vis = {}
         hs = {}
         pst = {}
-        prs = {}
+
+        def acc_of(i):
+            return ACC_EARLY if blocks[i][0] < B_SPLIT else ACC_LATE
 
         def load(i):
             b0, nb = blocks[i]
@@ -259,7 +261,7 @@ def tile_attentionmechanism_pa_t_kernel(tc, v_i, v_q, l1_w, l1_b, w_vi0, w_u0, b
                         func=FUNC.Tanh,
                         bias=vqb[:, m, b0 + b : b0 + b + 1],
                     )
-                if m < ACC_CHUNKS:
+                if m < acc_of(i):
                     for b in range(nb):
                         nc.scalar.activation(
                             out=h[:, m, b * S : (b + 1) * S],
@@ -270,36 +272,26 @@ def tile_attentionmechanism_pa_t_kernel(tc, v_i, v_q, l1_w, l1_b, w_vi0, w_u0, b
                 else:
                     nc.scalar.activation(out=h[:, m, :cols], in_=h[:, m, :cols], func=FUNC.Exp)
 
-        def prod(i):
+        def wsum(i):
             b0, nb = blocks[i]
             cols = nb * S
             h = hs[i]
             vi = vis[i]
-            pr = prp.tile([P, NCH, HPAD], F32, name="pr")
-            prs[i] = pr
-            nv = NCH if i == nblk - 1 else NCH - POOL_CHUNKS
-            for m in range(nv, NCH):
-                nc.gpsimd.tensor_tensor(out=pr[:, m, :cols], in0=h[:, m, :cols], in1=vi[:, m, :cols], op=ALU.mult)
-            if nv > 0:
-                nc.vector.tensor_tensor(out=pr[:, :nv, :cols], in0=h[:, :nv, :cols], in1=vi[:, :nv, :cols], op=ALU.mult)
-
-        def sume(i):
-            b0, nb = blocks[i]
-            cols = nb * S
-            if ACC_CHUNKS < NCH:
+            nv = NCH - POOL_CHUNKS
+            acc = acc_of(i)
+            if acc < NCH:
                 nc.vector.tensor_reduce(
-                    out=den[:, ACC_CHUNKS:, b0 : b0 + nb],
-                    in_=hs[i][:, ACC_CHUNKS:, :cols].rearrange("p m (b s) -> p m b s", s=S),
+                    out=den[:, acc:, b0 : b0 + nb],
+                    in_=h[:, acc:, :cols].rearrange("p m (b s) -> p m b s", s=S),
                     axis=AXIS.X,
                     op=ALU.add,
                 )
-
-        def sump(i):
-            b0, nb = blocks[i]
-            cols = nb * S
+            for m in range(nv, NCH):
+                nc.gpsimd.tensor_tensor(out=h[:, m, :cols], in0=h[:, m, :cols], in1=vi[:, m, :cols], op=ALU.mult)
+            nc.vector.tensor_tensor(out=h[:, :nv, :cols], in0=h[:, :nv, :cols], in1=vi[:, :nv, :cols], op=ALU.mult)
             nc.vector.tensor_reduce(
                 out=num[:, :, b0 : b0 + nb],
-                in_=prs[i][:, :, :cols].rearrange("p m (b s) -> p m b s", s=S),
+                in_=h[:, :, :cols].rearrange("p m (b s) -> p m b s", s=S),
                 axis=AXIS.X,
                 op=ALU.add,
             )
@@ -353,7 +345,7 @@ def tile_attentionmechanism_pa_t_kernel(tc, v_i, v_q, l1_w, l1_b, w_vi0, w_u0, b
         wq("w3", 0)
         mm3()
         wq("w2", 0)
-        for k in range(nblk + 2):
+        for k in range(nblk + 1):
             if 1 <= k and k + 2 < nblk:
                 load(k + 2)
             if k + 2 < nblk:
@@ -366,12 +358,9 @@ def tile_attentionmechanism_pa_t_kernel(tc, v_i, v_q, l1_w, l1_b, w_vi0, w_u0, b
                 mm2(k)
             if k + 2 < nblk:
                 mm1(k + 2)
-            if k >= 2:
-                sump(k - 2)
-            if k == nblk:
+            if k >= 1:
+                wsum(k - 1)
+            if k == nblk - 1:
                 ratio(0, blocks[nblk - 1][0])
-            if 1 <= k <= nblk:
-                prod(k - 1)
-                sume(k - 1)
         ratio(blocks[nblk - 1][0], B)
         finish()

@@ -21,9 +21,7 @@ HPAD = 496
 FLOPS = 2 * B * S * C * HID + 2 * B * S * HID * HID + 2 * B * HID * HID
 
 SIZES = [10] * 12 + [8]
-ACC_EARLY = 4
-ACC_LATE = 0
-B_SPLIT = 80
+ACC_CHUNKS = 4
 POOL_CHUNKS = 0
 RUN4 = False
 RX_ACT = {}
@@ -97,9 +95,6 @@ def tile_attentionmechanism_pa_t_kernel(tc, v_i, v_q, l1_w, l1_b, w_vi0, w_u0, b
         vis = {}
         hs = {}
         pst = {}
-
-        def acc_of(i):
-            return ACC_EARLY if blocks[i][0] < B_SPLIT else ACC_LATE
 
         def load(i):
             b0, nb = blocks[i]
@@ -261,7 +256,7 @@ def tile_attentionmechanism_pa_t_kernel(tc, v_i, v_q, l1_w, l1_b, w_vi0, w_u0, b
                         func=FUNC.Tanh,
                         bias=vqb[:, m, b0 + b : b0 + b + 1],
                     )
-                if m < acc_of(i):
+                if m < ACC_CHUNKS:
                     for b in range(nb):
                         nc.scalar.activation(
                             out=h[:, m, b * S : (b + 1) * S],
@@ -272,26 +267,17 @@ def tile_attentionmechanism_pa_t_kernel(tc, v_i, v_q, l1_w, l1_b, w_vi0, w_u0, b
                 else:
                     nc.scalar.activation(out=h[:, m, :cols], in_=h[:, m, :cols], func=FUNC.Exp)
 
-        def wsum(i):
+        def prod(i):
             b0, nb = blocks[i]
             cols = nb * S
-            h = hs[i]
-            vi = vis[i]
-            nv = NCH - POOL_CHUNKS
-            acc = acc_of(i)
-            if acc < NCH:
-                nc.vector.tensor_reduce(
-                    out=den[:, acc:, b0 : b0 + nb],
-                    in_=h[:, acc:, :cols].rearrange("p m (b s) -> p m b s", s=S),
-                    axis=AXIS.X,
-                    op=ALU.add,
-                )
-            for m in range(nv, NCH):
-                nc.gpsimd.tensor_tensor(out=h[:, m, :cols], in0=h[:, m, :cols], in1=vi[:, m, :cols], op=ALU.mult)
-            nc.vector.tensor_tensor(out=h[:, :nv, :cols], in0=h[:, :nv, :cols], in1=vi[:, :nv, :cols], op=ALU.mult)
+            nc.vector.tensor_tensor(out=hs[i][:, :, :cols], in0=hs[i][:, :, :cols], in1=vis[i][:, :, :cols], op=ALU.mult)
+
+        def sump(i):
+            b0, nb = blocks[i]
+            cols = nb * S
             nc.vector.tensor_reduce(
                 out=num[:, :, b0 : b0 + nb],
-                in_=h[:, :, :cols].rearrange("p m (b s) -> p m b s", s=S),
+                in_=hs[i][:, :, :cols].rearrange("p m (b s) -> p m b s", s=S),
                 axis=AXIS.X,
                 op=ALU.add,
             )
@@ -350,16 +336,20 @@ def tile_attentionmechanism_pa_t_kernel(tc, v_i, v_q, l1_w, l1_b, w_vi0, w_u0, b
                 load(k + 2)
             if k + 2 < nblk:
                 rx(k + 2)
-                qx(k + 2)
             if k + 1 < nblk:
                 v(k + 1)
+            if k + 2 < nblk:
+                qx(k + 2)
+            if k >= 1:
+                prod(k - 1)
+            if k + 1 < nblk:
                 qv(k + 1)
+            if k >= 1:
+                sump(k - 1)
             if k < nblk:
                 mm2(k)
             if k + 2 < nblk:
                 mm1(k + 2)
-            if k >= 1:
-                wsum(k - 1)
             if k == nblk - 1:
                 ratio(0, blocks[nblk - 1][0])
         ratio(blocks[nblk - 1][0], B)

@@ -28,7 +28,8 @@ RX_ACT = {}
 MANUAL = True
 RAW_BUFS = 3
 VI_BUFS = 5
-H_BUFS = 3
+H_BUFS = 4
+FOLD_COUNTS = [49, 25, 13, 7, 4, 2]
 
 
 def tile_attentionmechanism_pa_t_kernel(tc, v_i, v_q, l1_w, l1_b, w_vi0, w_u0, b_u0, out):
@@ -141,9 +142,13 @@ def tile_attentionmechanism_pa_t_kernel(tc, v_i, v_q, l1_w, l1_b, w_vi0, w_u0, b
             )
 
         def rx(i):
+            rxh(i, 0)
+            rxh(i, 1)
+
+        def rxh(i, g):
             b0, nb = blocks[i]
             raw = raws[i]
-            for g in range(2):
+            if True:
                 dst = xg[i % 2][:, g, : nb * S, :].rearrange("p (b s) t -> p b s t", s=S)
                 src = raw[g][:, :nb, :].rearrange("p b (t s) -> p b t s", t=4)
                 if RX_ACT.get(i, 0) > g:
@@ -272,15 +277,18 @@ def tile_attentionmechanism_pa_t_kernel(tc, v_i, v_q, l1_w, l1_b, w_vi0, w_u0, b
             cols = nb * S
             nc.vector.tensor_tensor(out=hs[i][:, :, :cols], in0=hs[i][:, :, :cols], in1=vis[i][:, :, :cols], op=ALU.mult)
 
-        def sump(i):
+        def fold(i, level):
             b0, nb = blocks[i]
-            cols = nb * S
-            nc.vector.tensor_reduce(
-                out=num[:, :, b0 : b0 + nb],
-                in_=hs[i][:, :, :cols].rearrange("p m (b s) -> p m b s", s=S),
-                axis=AXIS.X,
-                op=ALU.add,
-            )
+            x = hs[i][:, :, : nb * S].rearrange("p m (b s) -> p m b s", s=S)
+            count = FOLD_COUNTS[level]
+            half = count // 2
+            keep = count - half
+            if count == 2:
+                nc.vector.tensor_tensor(out=num[:, :, b0 : b0 + nb], in0=x[:, :, :, 0], in1=x[:, :, :, 1], op=ALU.add)
+            else:
+                nc.vector.tensor_tensor(
+                    out=x[:, :, :, :half], in0=x[:, :, :, :half], in1=x[:, :, :, keep:count], op=ALU.add
+                )
 
         def ratio(lo, hi):
             nc.vector.reciprocal(out=rden[:, :, lo:hi], in_=den[:, :, lo:hi])
@@ -331,26 +339,28 @@ def tile_attentionmechanism_pa_t_kernel(tc, v_i, v_q, l1_w, l1_b, w_vi0, w_u0, b
         wq("w3", 0)
         mm3()
         wq("w2", 0)
-        for k in range(nblk + 1):
+        for k in range(nblk + 2):
             if 1 <= k and k + 2 < nblk:
                 load(k + 2)
+            front = [lambda: None] * 6
             if k + 2 < nblk:
-                rx(k + 2)
+                front[0] = lambda: rxh(k + 2, 0)
+                front[1] = lambda: rxh(k + 2, 1)
+                front[3] = lambda: qx(k + 2)
             if k + 1 < nblk:
-                v(k + 1)
-            if k + 2 < nblk:
-                qx(k + 2)
-            if k >= 1:
-                prod(k - 1)
-            if k + 1 < nblk:
-                qv(k + 1)
-            if k >= 1:
-                sump(k - 1)
+                front[2] = lambda: v(k + 1)
+                front[5] = lambda: qv(k + 1)
+            if 1 <= k <= nblk:
+                front[4] = lambda: prod(k - 1)
+            for level in range(6):
+                front[level]()
+                if k >= 2:
+                    fold(k - 2, level)
             if k < nblk:
                 mm2(k)
             if k + 2 < nblk:
                 mm1(k + 2)
-            if k == nblk - 1:
+            if k == nblk:
                 ratio(0, blocks[nblk - 1][0])
         ratio(blocks[nblk - 1][0], B)
         finish()

@@ -23,13 +23,12 @@ FLOPS = 2 * B * S * C * HID + 2 * B * S * HID * HID + 2 * B * HID * HID
 SIZES = [10] * 12 + [8]
 ACC_CHUNKS = 4
 POOL_CHUNKS = 0
-RUN4 = False
+RUN4 = True
 RX_ACT = {}
 MANUAL = True
 RAW_BUFS = 3
 VI_BUFS = 5
-H_BUFS = 4
-FOLD_COUNTS = [49, 25, 13, 7, 4, 2]
+H_BUFS = 3
 
 
 def tile_attentionmechanism_pa_t_kernel(tc, v_i, v_q, l1_w, l1_b, w_vi0, w_u0, b_u0, out):
@@ -142,23 +141,18 @@ def tile_attentionmechanism_pa_t_kernel(tc, v_i, v_q, l1_w, l1_b, w_vi0, w_u0, b
             )
 
         def rx(i):
-            rxh(i, 0)
-            rxh(i, 1)
-
-        def rxh(i, g):
             b0, nb = blocks[i]
             raw = raws[i]
-            if True:
+            for g in range(2):
                 dst = xg[i % 2][:, g, : nb * S, :].rearrange("p (b s) t -> p b s t", s=S)
                 src = raw[g][:, :nb, :].rearrange("p b (t s) -> p b t s", t=4)
                 if RX_ACT.get(i, 0) > g:
                     nc.scalar.copy(out=dst, in_=src.rearrange("p b t s -> p b s t"))
                 elif RUN4:
                     nc.vector.tensor_copy(
-                        out=dst[:, :, :48, :].rearrange("p b (c i) t -> p b c t i", i=4),
-                        in_=src[:, :, :, :48].rearrange("p b t (c i) -> p b c t i", i=4),
+                        out=dst.rearrange("p b (c i) t -> p b c t i", i=7),
+                        in_=src.rearrange("p b t (c i) -> p b c t i", i=7),
                     )
-                    nc.vector.tensor_copy(out=dst[:, :, 48, :], in_=src[:, :, :, 48])
                 else:
                     nc.vector.tensor_copy(out=dst, in_=src.rearrange("p b t s -> p b s t"))
 
@@ -277,18 +271,15 @@ def tile_attentionmechanism_pa_t_kernel(tc, v_i, v_q, l1_w, l1_b, w_vi0, w_u0, b
             cols = nb * S
             nc.vector.tensor_tensor(out=hs[i][:, :, :cols], in0=hs[i][:, :, :cols], in1=vis[i][:, :, :cols], op=ALU.mult)
 
-        def fold(i, level):
+        def sump(i):
             b0, nb = blocks[i]
-            x = hs[i][:, :, : nb * S].rearrange("p m (b s) -> p m b s", s=S)
-            count = FOLD_COUNTS[level]
-            half = count // 2
-            keep = count - half
-            if count == 2:
-                nc.vector.tensor_tensor(out=num[:, :, b0 : b0 + nb], in0=x[:, :, :, 0], in1=x[:, :, :, 1], op=ALU.add)
-            else:
-                nc.vector.tensor_tensor(
-                    out=x[:, :, :, :half], in0=x[:, :, :, :half], in1=x[:, :, :, keep:count], op=ALU.add
-                )
+            cols = nb * S
+            nc.vector.tensor_reduce(
+                out=num[:, :, b0 : b0 + nb],
+                in_=hs[i][:, :, :cols].rearrange("p m (b s) -> p m b s", s=S),
+                axis=AXIS.X,
+                op=ALU.add,
+            )
 
         def ratio(lo, hi):
             nc.vector.reciprocal(out=rden[:, :, lo:hi], in_=den[:, :, lo:hi])
@@ -339,28 +330,26 @@ def tile_attentionmechanism_pa_t_kernel(tc, v_i, v_q, l1_w, l1_b, w_vi0, w_u0, b
         wq("w3", 0)
         mm3()
         wq("w2", 0)
-        for k in range(nblk + 2):
+        for k in range(nblk + 1):
             if 1 <= k and k + 2 < nblk:
                 load(k + 2)
-            front = [lambda: None] * 6
             if k + 2 < nblk:
-                front[0] = lambda: rxh(k + 2, 0)
-                front[1] = lambda: rxh(k + 2, 1)
-                front[3] = lambda: qx(k + 2)
+                rx(k + 2)
             if k + 1 < nblk:
-                front[2] = lambda: v(k + 1)
-                front[5] = lambda: qv(k + 1)
-            if 1 <= k <= nblk:
-                front[4] = lambda: prod(k - 1)
-            for level in range(6):
-                front[level]()
-                if k >= 2:
-                    fold(k - 2, level)
+                v(k + 1)
+            if k + 2 < nblk:
+                qx(k + 2)
+            if k >= 1:
+                prod(k - 1)
+            if k + 1 < nblk:
+                qv(k + 1)
+            if k >= 1:
+                sump(k - 1)
             if k < nblk:
                 mm2(k)
             if k + 2 < nblk:
                 mm1(k + 2)
-            if k == nblk:
+            if k == nblk - 1:
                 ratio(0, blocks[nblk - 1][0])
         ratio(blocks[nblk - 1][0], B)
         finish()

@@ -7,7 +7,6 @@ F32 = mybir.dt.float32
 BF16 = mybir.dt.bfloat16
 U32 = mybir.dt.uint32
 U8 = mybir.dt.uint8
-I32 = mybir.dt.int32
 FP8X4 = mybir.dt.float8_e4m3fn_x4
 FUNC = mybir.ActivationFunctionType
 ALU = mybir.AluOpType
@@ -16,102 +15,80 @@ AXIS = mybir.AxisListType
 B, C, S, T, HID = 128, 1024, 49, 20, 512
 P = 128
 NCH = 4
-NCOL = 512
-HPAD = 496
+NT = 7
+TB = 18
+RUN = 7
+KK = 7
+COLS = KK * P
 FLOPS = 2 * B * S * C * HID + 2 * B * S * HID * HID + 2 * B * HID * HID
-
-SIZES = [10] * 12 + [8]
-ACC_CHUNKS = 4
-POOL_CHUNKS = 0
-RUN4 = True
-RX_ACT = {}
-MANUAL = True
-RAW_BUFS = 3
-VI_BUFS = 5
-H_BUFS = 3
 
 
 def tile_attentionmechanism_pa_t_kernel(tc, v_i, v_q, l1_w, l1_b, w_vi0, w_u0, b_u0, out):
     nc = tc.nc
-    nblk = len(SIZES)
-    blocks = [(sum(SIZES[:i]), SIZES[i]) for i in range(nblk)]
-    nbmax = max(SIZES)
 
     with ExitStack() as ctx:
         keep = ctx.enter_context(tc.tile_pool(name="keep", bufs=1))
-        rawp = ctx.enter_context(tc.tile_pool(name="rawp", bufs=RAW_BUFS))
-        vip = ctx.enter_context(tc.tile_pool(name="vip", bufs=VI_BUFS))
-        hp = ctx.enter_context(tc.tile_pool(name="hp", bufs=H_BUFS))
-        ps1 = ctx.enter_context(tc.psum_pool(name="ps1", bufs=4))
-        ps2 = ctx.enter_context(tc.psum_pool(name="ps2", bufs=4))
-        if MANUAL:
-            ctx.enter_context(tc.manual_schedule())
+        rawp = ctx.enter_context(tc.tile_pool(name="rawp", bufs=2))
+        vip = ctx.enter_context(tc.tile_pool(name="vip", bufs=3))
+        sjp = ctx.enter_context(tc.tile_pool(name="sjp", bufs=2))
+        ps1 = ctx.enter_context(tc.psum_pool(name="ps1", bufs=3))
+        ps2 = ctx.enter_context(tc.psum_pool(name="ps2", bufs=3))
+        pst = ctx.enter_context(tc.psum_pool(name="pst", bufs=2))
+        ctx.enter_context(tc.manual_schedule())
 
-        xg = [keep.tile([P, 2, NCOL, 4], BF16, align_bytes=64, name="xg%d" % i) for i in range(2)]
-        xq = [keep.tile([P, 2, NCOL], U32, align_bytes=64, name="xq%d" % i) for i in range(2)]
-        xs = [keep.tile([P, 2, NCOL], U8, align_bytes=64, name="xs%d" % i) for i in range(2)]
-        vg = [keep.tile([P, NCOL, 4], BF16, align_bytes=64, name="vg%d" % i) for i in range(2)]
-        vc = [keep.tile([P, NCOL], U32, align_bytes=64, name="vc%d" % i) for i in range(2)]
-        vs = [keep.tile([P, NCOL], U8, align_bytes=64, name="vs%d" % i) for i in range(2)]
-        for i in range(2):
-            nc.vector.memset(xg[i][:].rearrange("p g c t -> p (g c t)").bitcast(I32), 0)
-            nc.vector.memset(vg[i][:].rearrange("p c t -> p (c t)").bitcast(I32), 0)
+        xg = keep.tile([P, 2, COLS, 4], BF16, align_bytes=64, name="xg")
+        xq = [keep.tile([P, 2, COLS], U32, align_bytes=64, name="xq%d" % i) for i in range(2)]
+        xs = [keep.tile([P, 2, COLS], U8, align_bytes=64, name="xs%d" % i) for i in range(2)]
+        vg = keep.tile([P, COLS, 4], BF16, align_bytes=64, name="vg")
+        vc = [keep.tile([P, COLS], U32, align_bytes=64, name="vc%d" % i) for i in range(2)]
+        vs = [keep.tile([P, COLS], U8, align_bytes=64, name="vs%d" % i) for i in range(2)]
+        rawx = [keep.tile([P, 2, 4 * S], BF16, name="rawx%d" % g) for g in range(2)]
 
         ident32 = keep.tile([P, P], F32, name="ident32")
         make_identity(nc, ident32[:])
         identb = keep.tile([P, P], BF16, name="identb")
         make_identity(nc, identb[:])
 
-        wraw = {
-            "w1": keep.tile([P, NCH, C], BF16, name="w1raw"),
-            "w2": keep.tile([P, NCH, HID], BF16, name="w2raw"),
-            "w3": keep.tile([P, NCH, HID], BF16, name="w3raw"),
-        }
         wsrc = {"w1": l1_w, "w2": w_vi0, "w3": w_u0}
         wpass = {"w1": 2, "w2": 1, "w3": 1}
-        wgrp = {}
         wq_ = {}
         ws_ = {}
         for nm in ("w1", "w2", "w3"):
-            wgrp[nm] = keep.tile([P, wpass[nm], NCH, P, 4], BF16, align_bytes=64, name=nm + "g")
             wq_[nm] = keep.tile([P, wpass[nm], NCH * P], U32, align_bytes=64, name=nm + "q")
             ws_[nm] = keep.tile([P, wpass[nm], NCH * P], U8, align_bytes=64, name=nm + "s")
-        vqr = keep.tile([P, T, HID], BF16, name="vqr")
         l1b_raw = keep.tile([P, NCH], BF16, name="l1b_raw")
         bu_raw = keep.tile([P, NCH], BF16, name="bu_raw")
         l1b = keep.tile([P, NCH], F32, name="l1b")
         bu = keep.tile([P, NCH], F32, name="bu")
         u32 = keep.tile([P, NCH, P], F32, name="u32")
-        ug = keep.tile([P, B, 4], BF16, align_bytes=64, name="ug")
-        uq = keep.tile([P, B], U32, align_bytes=64, name="uq")
-        us = keep.tile([P, B], U8, align_bytes=64, name="us")
-        vqb = keep.tile([P, NCH, B], F32, name="vqb")
-        num = keep.tile([P, NCH, B], F32, name="num")
-        den = keep.tile([P, NCH, B], F32, name="den")
-        rden = keep.tile([P, NCH, B], F32, name="rden")
+        uq = keep.tile([P, NT * P], U32, align_bytes=64, name="uq")
+        us = keep.tile([P, NT * P], U8, align_bytes=64, name="us")
+        sums = {nd: keep.tile([P, NCH, B], F32, name="sum_" + nd) for nd in ("num", "den")}
+        tail = {nd: keep.tile([P, NCH, 2, NT], F32, name="tail_" + nd) for nd in ("num", "den")}
         osb = keep.tile([P, P, NCH], F32, name="osb")
 
         raws = {}
         vis = {}
-        hs = {}
-        pst = {}
+        es = {}
+        pts = {}
+        sjs = {}
+        pbs = {}
+        pst_u = {}
 
         def load(i):
-            b0, nb = blocks[i]
-            raw = [rawp.tile([P, nbmax, 4 * S], BF16, name="raw%d" % g) for g in range(2)]
+            raws[i] = [rawp.tile([P, TB, 4 * S], BF16, name="raw%d" % g) for g in range(2)]
             for g in range(2):
                 nc.sync.dma_start(
-                    out=raw[g][:, :nb, :],
-                    in_=v_i[b0 : b0 + nb, g * 512 : (g + 1) * 512].rearrange("b (p t) h w -> p b (t h w)", t=4),
+                    out=raws[i][g][:],
+                    in_=v_i[TB * i : TB * (i + 1), g * 512 : (g + 1) * 512].rearrange("b (p t) h w -> p b (t h w)", t=4),
                 )
-            raws[i] = raw
 
-        def loadw(nm):
-            nc.sync.dma_start(out=wraw[nm][:], in_=wsrc[nm].rearrange("(j m) k -> j m k", m=NCH))
-
-        def loadvq():
-            for c in range(4):
-                nc.sync.dma_start(out=vqr[:, 5 * c : 5 * c + 5, :], in_=v_q[:, 5 * c : 5 * c + 5, :])
+        def loadx():
+            for g in range(2):
+                nc.sync.dma_start(
+                    out=rawx[g][:],
+                    in_=v_i[TB * NT : B, g * 512 : (g + 1) * 512].rearrange("b (p t) h w -> p b (t h w)", t=4),
+                )
 
         def loadb():
             nc.scalar.dma_start(out=l1b_raw[:], in_=l1_b.rearrange("(j m) -> j m", m=NCH))
@@ -121,174 +98,124 @@ def tile_attentionmechanism_pa_t_kernel(tc, v_i, v_q, l1_w, l1_b, w_vi0, w_u0, b
             nc.vector.tensor_copy(out=l1b[:], in_=l1b_raw[:])
             nc.vector.tensor_copy(out=bu[:], in_=bu_raw[:])
 
-        def wt(nm, g):
-            for mh in range(2):
-                pt = ps1.tile([P, 2, 2, P], F32, name="pt", tag="ps1")
-                for mm in range(2):
-                    words = wraw[nm][:, 2 * mh + mm, :].bitcast(F32).rearrange("p (g q u) -> p g u q", g=wpass[nm], u=2)
-                    for u in range(2):
-                        nc.tensor.transpose(pt[:, mm, u, :], words[:, g, u, :], ident32[:])
-                nc.scalar.copy(
-                    out=wgrp[nm][:, g, 2 * mh : 2 * mh + 2, :, :].bitcast(F32),
-                    in_=pt[:].rearrange("p a u j -> p a j u"),
-                )
-
-        def wq(nm, g):
-            nc.vector.quantize_mx(
-                out=wq_[nm][:, g, :].bitcast(FP8X4),
-                scales=ws_[nm][:, g, :],
-                in_=wgrp[nm][:, g].rearrange("p m j t -> p (m j t)"),
+        def rx(i, g):
+            dst = xg[:, g].rearrange("p (k c) t -> p k c t", c=P)
+            nc.vector.tensor_copy(
+                out=dst[:, :, 0 : TB * RUN, :].rearrange("p k (b r) t -> p b k t r", r=RUN),
+                in_=raws[i][g][:].rearrange("p b (t k r) -> p b k t r", t=4, r=RUN),
+            )
+            nc.vector.tensor_copy(
+                out=dst[:, :, TB * RUN : P, :].rearrange("p k x t -> p x k t"),
+                in_=rawx[g][:].rearrange("p x (t k r) -> p x k t r", t=4, r=RUN)[:, :, :, :, i],
             )
 
-        def rx(i):
-            b0, nb = blocks[i]
-            raw = raws[i]
-            for g in range(2):
-                dst = xg[i % 2][:, g, : nb * S, :].rearrange("p (b s) t -> p b s t", s=S)
-                src = raw[g][:, :nb, :].rearrange("p b (t s) -> p b t s", t=4)
-                if RX_ACT.get(i, 0) > g:
-                    nc.scalar.copy(out=dst, in_=src.rearrange("p b t s -> p b s t"))
-                elif RUN4:
-                    nc.vector.tensor_copy(
-                        out=dst.rearrange("p b (c i) t -> p b c t i", i=7),
-                        in_=src.rearrange("p b t (c i) -> p b c t i", i=7),
-                    )
-                else:
-                    nc.vector.tensor_copy(out=dst, in_=src.rearrange("p b t s -> p b s t"))
+        def quant(codes, scales, src):
+            for lo, hi in ((0, 512), (512, 768), (768, 896)):
+                nc.vector.quantize_mx(
+                    out=codes[:, lo:hi].bitcast(FP8X4),
+                    scales=scales[:, lo:hi],
+                    in_=src[:, lo:hi, :].rearrange("p c t -> p (c t)"),
+                )
 
         def qx(i):
-            nc.vector.quantize_mx(
-                out=xq[i % 2][:].rearrange("p g c -> p (g c)").bitcast(FP8X4),
-                scales=xs[i % 2][:].rearrange("p g c -> p (g c)"),
-                in_=xg[i % 2][:].rearrange("p g c t -> p (g c t)"),
+            for g in range(2):
+                quant(xq[i % 2][:, g], xs[i % 2][:, g], xg[:, g])
+
+        def mx(ps, o, n, w, g, m, codes, scales, c, start, stop):
+            nc.tensor.matmul_mx(
+                out=ps[:, o : o + n],
+                lhsT=wq_[w][:, g, m * P : (m + 1) * P].bitcast(FP8X4),
+                lhsT_scale=ws_[w][:, g, m * P : (m + 1) * P],
+                rhs=codes[:, c : c + n].bitcast(FP8X4),
+                rhs_scale=scales[:, c : c + n],
+                start=start,
+                stop=stop,
             )
 
-        def mm1(i):
-            b0, nb = blocks[i]
-            cols = nb * S
-            vi = vip.tile([P, NCH, nbmax * S], F32, name="vi")
-            vis[i] = vi
-            for m in range(NCH):
-                ps = ps1.tile([P, NCOL], F32, name="ps", tag="ps1")
-                for g in range(2):
-                    nc.tensor.matmul_mx(
-                        out=ps[:],
-                        lhsT=wq_["w1"][:, g, m * P : (m + 1) * P].bitcast(FP8X4),
-                        lhsT_scale=ws_["w1"][:, g, m * P : (m + 1) * P],
-                        rhs=xq[i % 2][:, g, :].bitcast(FP8X4),
-                        rhs_scale=xs[i % 2][:, g, :],
-                        start=(g == 0),
-                        stop=(g == 1),
-                    )
-                nc.scalar.activation(out=vi[:, m, :cols], in_=ps[:, :cols], func=FUNC.Tanh, bias=l1b[:, m : m + 1])
+        def mm1(i, m):
+            if m == 0:
+                vis[i] = vip.tile([P, NCH, COLS], F32, name="vi")
+            for lo, pieces in ((0, ((0, 512),)), (512, ((0, 256), (256, 128)))):
+                ps = ps1.tile([P, 512], F32, name="ps", tag="ps1")
+                for o, n in pieces:
+                    for g in range(2):
+                        mx(ps, o, n, "w1", g, m, xq[i % 2][:, g], xs[i % 2][:, g], lo + o, g == 0, g == 1)
+                w = sum(n for o, n in pieces)
+                nc.scalar.activation(
+                    out=vis[i][:, m, lo : lo + w], in_=ps[:, :w], func=FUNC.Tanh, bias=l1b[:, m : m + 1]
+                )
 
         def v(i):
-            b0, nb = blocks[i]
-            cols = nb * S
-            nc.vector.tensor_copy(out=vg[i % 2][:, :cols, :], in_=vis[i][:, :, :cols].rearrange("p m c -> p c m"))
+            nc.vector.tensor_copy(out=vg[:], in_=vis[i][:].rearrange("p m c -> p c m"))
 
         def qv(i):
-            nc.vector.quantize_mx(
-                out=vc[i % 2][:].bitcast(FP8X4),
-                scales=vs[i % 2][:],
-                in_=vg[i % 2][:].rearrange("p c t -> p (c t)"),
+            quant(vc[i % 2], vs[i % 2], vg)
+
+        def mm2(i, m):
+            if m == 0:
+                es[i] = late.tile([P, NCH, COLS], F32, name="e")
+            for lo, pieces in ((0, ((0, 512),)), (512, ((0, 256), (256, 128)))):
+                ps = ps2.tile([P, 512], F32, name="pz", tag="ps2")
+                for o, n in pieces:
+                    mx(ps, o, n, "w2", 0, m, vc[i % 2], vs[i % 2], lo + o, True, False)
+                    for q in range(o, o + n, P):
+                        mx(ps, q, P, "w3", 0, m, uq, us, i * P, False, q + P == o + n)
+                w = sum(n for o, n in pieces)
+                nc.scalar.activation(
+                    out=es[i][:, m, lo : lo + w], in_=ps[:, :w], func=FUNC.Tanh, bias=bu[:, m : m + 1]
+                )
+
+        def ex(i, lo, hi):
+            nc.scalar.activation(out=es[i][:, lo:hi, :], in_=es[i][:, lo:hi, :], func=FUNC.Exp)
+
+        def prod(i, lo, hi):
+            nc.vector.tensor_tensor(
+                out=vis[i][:, lo:hi, :], in0=es[i][:, lo:hi, :], in1=vis[i][:, lo:hi, :], op=ALU.mult
             )
 
-        def uc(c):
-            if c == 0:
-                pst["pu"] = ps2.tile([P, HID], F32, name="pu", tag="ps2")
-            for t in range(5 * c, 5 * c + 5):
-                nc.tensor.matmul(pst["pu"][:], lhsT=identb[:], rhs=vqr[:, t, :], start=(t == 0), stop=(t == T - 1))
-
-        def usc():
-            nc.scalar.activation(
-                out=u32[:], in_=pst["pu"][:].rearrange("b (j m) -> b m j", m=NCH), func=FUNC.Copy, scale=1.0 / T
-            )
-            pst["put"] = ps2.tile([P, NCH, P], F32, name="put", tag="ps2")
-            for m in range(NCH):
-                nc.tensor.transpose(pst["put"][:, m, :], u32[:, m, :], ident32[:])
-
-        def ugr():
-            nc.vector.tensor_copy(out=ug[:], in_=pst["put"][:].rearrange("j m b -> j b m"))
-
-        def uqu():
-            nc.vector.quantize_mx(out=uq[:].bitcast(FP8X4), scales=us[:], in_=ug[:].rearrange("p b t -> p (b t)"))
-
-        def mm3():
-            pv = ps2.tile([P, NCH, P], F32, name="pv", tag="ps2")
-            for m in range(NCH):
-                nc.tensor.matmul_mx(
-                    out=pv[:, m, :],
-                    lhsT=wq_["w3"][:, 0, m * P : (m + 1) * P].bitcast(FP8X4),
-                    lhsT_scale=ws_["w3"][:, 0, m * P : (m + 1) * P],
-                    rhs=uq[:].bitcast(FP8X4),
-                    rhs_scale=us[:],
-                    start=True,
-                    stop=True,
-                )
-            for m in range(NCH):
-                nc.scalar.activation(out=vqb[:, m, :], in_=pv[:, m, :], func=FUNC.Identity, bias=bu[:, m : m + 1])
-
-        def mm2(i):
-            b0, nb = blocks[i]
-            cols = nb * S
-            h = hp.tile([P, NCH, HPAD], F32, name="h")
-            hs[i] = h
-            banks = []
-            for m in range(NCH):
-                ps = ps2.tile([P, NCOL], F32, name="pz", tag="ps2")
-                banks.append(ps)
-                nc.tensor.matmul_mx(
-                    out=ps[:],
-                    lhsT=wq_["w2"][:, 0, m * P : (m + 1) * P].bitcast(FP8X4),
-                    lhsT_scale=ws_["w2"][:, 0, m * P : (m + 1) * P],
-                    rhs=vc[i % 2][:].bitcast(FP8X4),
-                    rhs_scale=vs[i % 2][:],
-                    start=True,
-                    stop=True,
-                )
-            for m in range(NCH):
-                for b in range(nb):
-                    nc.scalar.activation(
-                        out=h[:, m, b * S : (b + 1) * S],
-                        in_=banks[m][:, b * S : (b + 1) * S],
-                        func=FUNC.Tanh,
-                        bias=vqb[:, m, b0 + b : b0 + b + 1],
+        def tr(i, nd, lo, hi):
+            data = es[i] if nd == "den" else vis[i]
+            if lo == 0:
+                pts[nd] = pst.tile([P, NCH, P], F32, name="pt", tag="pst")
+            for m in range(lo, hi):
+                for k in range(KK):
+                    nc.tensor.matmul(
+                        pts[nd][:, m, :],
+                        lhsT=data[:, m, k * P : (k + 1) * P],
+                        rhs=ident32[:],
+                        is_transpose=True,
+                        start=(k == 0),
+                        stop=(k == KK - 1),
                     )
-                if m < ACC_CHUNKS:
-                    for b in range(nb):
-                        nc.scalar.activation(
-                            out=h[:, m, b * S : (b + 1) * S],
-                            in_=h[:, m, b * S : (b + 1) * S],
-                            func=FUNC.Exp,
-                            accum_out=den[:, m, b0 + b : b0 + b + 1],
-                        )
-                else:
-                    nc.scalar.activation(out=h[:, m, :cols], in_=h[:, m, :cols], func=FUNC.Exp)
 
-        def prod(i):
-            b0, nb = blocks[i]
-            cols = nb * S
-            nc.vector.tensor_tensor(out=hs[i][:, :, :cols], in0=hs[i][:, :, :cols], in1=vis[i][:, :, :cols], op=ALU.mult)
+        def evac(nd):
+            sjs[nd] = sjp.tile([P, NCH, P], F32, name="sj_" + nd)
+            nc.scalar.copy(out=sjs[nd][:], in_=pts[nd][:])
 
-        def sump(i):
-            b0, nb = blocks[i]
-            cols = nb * S
+        def back(nd):
+            pbs[nd] = pst.tile([P, NCH, P], F32, name="pb", tag="pst")
+            for m in range(NCH):
+                nc.tensor.transpose(pbs[nd][:, m, :], sjs[nd][:, m, :], ident32[:])
+
+        def red(i, nd):
             nc.vector.tensor_reduce(
-                out=num[:, :, b0 : b0 + nb],
-                in_=hs[i][:, :, :cols].rearrange("p m (b s) -> p m b s", s=S),
+                out=sums[nd][:, :, TB * i : TB * (i + 1)],
+                in_=pbs[nd][:, :, 0 : TB * RUN].rearrange("p m (b r) -> p m b r", r=RUN),
                 axis=AXIS.X,
                 op=ALU.add,
             )
+            nc.vector.tensor_copy(out=tail[nd][:, :, :, i], in_=pbs[nd][:, :, TB * RUN : P])
 
-        def ratio(lo, hi):
-            nc.vector.reciprocal(out=rden[:, :, lo:hi], in_=den[:, :, lo:hi])
-            nc.vector.tensor_tensor(out=num[:, :, lo:hi], in0=num[:, :, lo:hi], in1=rden[:, :, lo:hi], op=ALU.mult)
+        def ratio():
+            for nd in ("den", "num"):
+                nc.vector.tensor_reduce(out=sums[nd][:, :, TB * NT : B], in_=tail[nd][:], axis=AXIS.X, op=ALU.add)
+            nc.vector.reciprocal(out=sums["den"][:], in_=sums["den"][:])
+            nc.vector.tensor_tensor(out=sums["num"][:], in0=sums["num"][:], in1=sums["den"][:], op=ALU.mult)
 
         def finish():
             po = ps1.tile([P, NCH, P], F32, name="po", tag="ps1")
             for m in range(NCH):
-                nc.tensor.transpose(po[:, m, :], num[:, m, :], ident32[:])
+                nc.tensor.transpose(po[:, m, :], sums["num"][:, m, :], ident32[:])
             nc.vector.tensor_tensor(
                 out=osb[:],
                 in0=po[:].rearrange("b m j -> b j m"),
@@ -297,59 +224,160 @@ def tile_attentionmechanism_pa_t_kernel(tc, v_i, v_q, l1_w, l1_b, w_vi0, w_u0, b
             )
             nc.sync.dma_start(out=out[:, :], in_=osb[:].rearrange("b j m -> b (j m)"))
 
-        loadb()
-        loadw("w1")
-        load(0)
-        load(1)
-        loadvq()
-        loadw("w3")
-        loadw("w2")
-        load(2)
-        castb()
-        wt("w1", 0)
-        wt("w1", 1)
-        rx(0)
-        wq("w1", 0)
-        wq("w1", 1)
-        qx(0)
-        mm1(0)
-        rx(1)
-        qx(1)
-        uc(0)
-        mm1(1)
-        uc(1)
-        uc(2)
-        uc(3)
-        usc()
-        wt("w3", 0)
-        wt("w2", 0)
-        v(0)
-        qv(0)
-        ugr()
-        uqu()
-        wq("w3", 0)
-        mm3()
-        wq("w2", 0)
-        for k in range(nblk + 1):
-            if 1 <= k and k + 2 < nblk:
-                load(k + 2)
-            if k + 2 < nblk:
-                rx(k + 2)
-            if k + 1 < nblk:
-                v(k + 1)
-            if k + 2 < nblk:
-                qx(k + 2)
-            if k >= 1:
-                prod(k - 1)
-            if k + 1 < nblk:
-                qv(k + 1)
-            if k >= 1:
-                sump(k - 1)
-            if k < nblk:
-                mm2(k)
-            if k + 2 < nblk:
-                mm1(k + 2)
-            if k == nblk - 1:
-                ratio(0, blocks[nblk - 1][0])
-        ratio(blocks[nblk - 1][0], B)
+        with tc.tile_pool(name="early", bufs=1) as early:
+            wraw = {}
+            wgrp = {}
+            for nm in ("w1", "w2", "w3"):
+                wraw[nm] = early.tile([P, NCH, 512 * wpass[nm]], BF16, name=nm + "raw")
+                wgrp[nm] = early.tile([P, wpass[nm], NCH, P, 4], BF16, align_bytes=64, name=nm + "g")
+            vqr = early.tile([P, T, HID], BF16, name="vqr")
+            ug = early.tile([P, B, 4], BF16, name="ug")
+            urep = early.tile([P, NT, P, 4], BF16, align_bytes=64, name="urep")
+
+            def loadw(nm):
+                nc.sync.dma_start(out=wraw[nm][:], in_=wsrc[nm].rearrange("(j m) k -> j m k", m=NCH))
+
+            def loadvq():
+                for c in range(4):
+                    nc.sync.dma_start(out=vqr[:, 5 * c : 5 * c + 5, :], in_=v_q[:, 5 * c : 5 * c + 5, :])
+
+            def wt(nm, g):
+                for mh in range(2):
+                    pt = ps1.tile([P, 2, 2, P], F32, name="pw", tag="ps1")
+                    for mm in range(2):
+                        words = wraw[nm][:, 2 * mh + mm, :].bitcast(F32).rearrange("p (g q u) -> p g u q", g=wpass[nm], u=2)
+                        for u in range(2):
+                            nc.tensor.transpose(pt[:, mm, u, :], words[:, g, u, :], ident32[:])
+                    nc.scalar.copy(
+                        out=wgrp[nm][:, g, 2 * mh : 2 * mh + 2, :, :].bitcast(F32),
+                        in_=pt[:].rearrange("p a u j -> p a j u"),
+                    )
+
+            def wq(nm, g):
+                nc.vector.quantize_mx(
+                    out=wq_[nm][:, g, :].bitcast(FP8X4),
+                    scales=ws_[nm][:, g, :],
+                    in_=wgrp[nm][:, g].rearrange("p m j t -> p (m j t)"),
+                )
+
+            def uc(c):
+                if c == 0:
+                    pst_u["pu"] = ps2.tile([P, HID], F32, name="pu", tag="ps2")
+                for t in range(5 * c, 5 * c + 5):
+                    nc.tensor.matmul(pst_u["pu"][:], lhsT=identb[:], rhs=vqr[:, t, :], start=(t == 0), stop=(t == T - 1))
+
+            def usc():
+                nc.scalar.activation(
+                    out=u32[:], in_=pst_u["pu"][:].rearrange("b (j m) -> b m j", m=NCH), func=FUNC.Copy, scale=1.0 / T
+                )
+                pst_u["put"] = ps2.tile([P, NCH, P], F32, name="put", tag="ps2")
+                for m in range(NCH):
+                    nc.tensor.transpose(pst_u["put"][:, m, :], u32[:, m, :], ident32[:])
+
+            def ugr():
+                nc.vector.tensor_copy(out=ug[:], in_=pst_u["put"][:].rearrange("j m b -> j b m"))
+
+            def urp():
+                nc.vector.tensor_copy(
+                    out=urep[:, :, 0 : TB * RUN, :].rearrange("p n (b r) t -> p n b r t", r=RUN),
+                    in_=ug[:, 0 : TB * NT, :]
+                    .rearrange("p (n b) t -> p n b t", n=NT)
+                    .unsqueeze(3)
+                    .to_broadcast([P, NT, TB, RUN, 4]),
+                )
+                nc.vector.tensor_copy(
+                    out=urep[:, :, TB * RUN : P, :],
+                    in_=ug[:, TB * NT : B, :].unsqueeze(1).to_broadcast([P, NT, 2, 4]),
+                )
+
+            def uqu():
+                quant(uq, us, urep[:].rearrange("p n c t -> p (n c) t"))
+
+            loadb()
+            loadw("w1")
+            loadx()
+            load(0)
+            load(1)
+            loadvq()
+            loadw("w3")
+            loadw("w2")
+            castb()
+            wt("w1", 0)
+            wt("w1", 1)
+            rx(0, 0)
+            wq("w1", 0)
+            rx(0, 1)
+            wq("w1", 1)
+            qx(0)
+            for m in range(NCH):
+                mm1(0, m)
+            rx(1, 0)
+            rx(1, 1)
+            for c in range(4):
+                uc(c)
+            usc()
+            wt("w3", 0)
+            wt("w2", 0)
+            v(0)
+            qx(1)
+            qv(0)
+            ugr()
+            wq("w3", 0)
+            urp()
+            wq("w2", 0)
+            uqu()
+
+        late = ctx.enter_context(tc.tile_pool(name="late", bufs=3))
+        for i in range(NT):
+            if i + 2 < NT:
+                load(i + 2)
+            if i + 1 < NT:
+                for m in range(NCH):
+                    mm1(i + 1, m)
+            if i >= 1:
+                prod(i - 1, 0, 2)
+                prod(i - 1, 2, 4)
+            if i >= 2:
+                back("den")
+                back("num")
+            for m in range(NCH):
+                mm2(i, m)
+            if i + 2 < NT:
+                rx(i + 2, 0)
+            if i + 1 < NT:
+                v(i + 1)
+            if i + 2 < NT:
+                rx(i + 2, 1)
+            if i + 1 < NT:
+                qv(i + 1)
+            if i >= 2:
+                red(i - 2, "den")
+                red(i - 2, "num")
+            if i + 2 < NT:
+                qx(i + 2)
+            ex(i, 0, 2)
+            if i >= 1:
+                tr(i - 1, "den", 0, NCH)
+                evac("den")
+            ex(i, 2, 4)
+            if i >= 1:
+                tr(i - 1, "num", 0, NCH)
+                evac("num")
+        last = NT - 1
+        back("den")
+        back("num")
+        prod(last, 0, 2)
+        prod(last, 2, 4)
+        red(last - 1, "den")
+        red(last - 1, "num")
+        tr(last, "den", 0, NCH)
+        evac("den")
+        tr(last, "num", 0, 2)
+        tr(last, "num", 2, 4)
+        evac("num")
+        back("den")
+        back("num")
+        red(last, "den")
+        red(last, "num")
+        ratio()
         finish()

@@ -20,6 +20,7 @@ TB = 18
 RUN = 7
 KK = 7
 COLS = KK * P
+HALVES = ((0, 512, ((0, 512),)), (512, 384, ((0, 256), (256, 128))))
 FLOPS = 2 * B * S * C * HID + 2 * B * S * HID * HID + 2 * B * HID * HID
 
 
@@ -39,9 +40,9 @@ def tile_attentionmechanism_pa_t_kernel(tc, v_i, v_q, l1_w, l1_b, w_vi0, w_u0, b
         xg = keep.tile([P, 2, COLS, 4], BF16, align_bytes=64, name="xg")
         xq = [keep.tile([P, 2, COLS], U32, align_bytes=64, name="xq%d" % i) for i in range(2)]
         xs = [keep.tile([P, 2, COLS], U8, align_bytes=64, name="xs%d" % i) for i in range(2)]
-        vg = keep.tile([P, COLS, 4], BF16, align_bytes=64, name="vg")
-        vc = [keep.tile([P, COLS], U32, align_bytes=64, name="vc%d" % i) for i in range(2)]
-        vs = [keep.tile([P, COLS], U8, align_bytes=64, name="vs%d" % i) for i in range(2)]
+        vg = [keep.tile([P, 512, 4], BF16, align_bytes=64, name="vg%d" % i) for i in range(2)]
+        vc = [keep.tile([P, 512], U32, align_bytes=64, name="vc%d" % i) for i in range(2)]
+        vs = [keep.tile([P, 512], U8, align_bytes=64, name="vs%d" % i) for i in range(2)]
         rawx = [keep.tile([P, 2, 4 * S], BF16, name="rawx%d" % g) for g in range(2)]
 
         ident32 = keep.tile([P, P], F32, name="ident32")
@@ -109,17 +110,18 @@ def tile_attentionmechanism_pa_t_kernel(tc, v_i, v_q, l1_w, l1_b, w_vi0, w_u0, b
                 in_=rawx[g][:].rearrange("p x (t k r) -> p x k t r", t=4, r=RUN)[:, :, :, :, i],
             )
 
-        def quant(codes, scales, src):
-            for lo, hi in ((0, 512), (512, 768), (768, 896)):
+        def quant(codes, scales, src, pieces):
+            for o, n in pieces:
                 nc.vector.quantize_mx(
-                    out=codes[:, lo:hi].bitcast(FP8X4),
-                    scales=scales[:, lo:hi],
-                    in_=src[:, lo:hi, :].rearrange("p c t -> p (c t)"),
+                    out=codes[:, o : o + n].bitcast(FP8X4),
+                    scales=scales[:, o : o + n],
+                    in_=src[:, o : o + n, :].rearrange("p c t -> p (c t)"),
                 )
 
-        def qx(i):
+        def qx(i, h):
+            lo, w, pieces = HALVES[h]
             for g in range(2):
-                quant(xq[i % 2][:, g], xs[i % 2][:, g], xg[:, g])
+                quant(xq[i % 2][:, g, lo : lo + w], xs[i % 2][:, g, lo : lo + w], xg[:, g, lo : lo + w, :], pieces)
 
         def mx(ps, o, n, w, g, m, codes, scales, c, start, stop):
             nc.tensor.matmul_mx(
@@ -132,46 +134,49 @@ def tile_attentionmechanism_pa_t_kernel(tc, v_i, v_q, l1_w, l1_b, w_vi0, w_u0, b
                 stop=stop,
             )
 
-        def mm1(i, m):
-            if m == 0:
+        def mm1(j, m):
+            i, h = divmod(j, 2)
+            lo, w, pieces = HALVES[h]
+            if h == 0 and m == 0:
                 vis[i] = vip.tile([P, NCH, COLS], F32, name="vi")
-            for lo, pieces in ((0, ((0, 512),)), (512, ((0, 256), (256, 128)))):
-                ps = ps1.tile([P, 512], F32, name="ps", tag="ps1")
-                for o, n in pieces:
-                    for g in range(2):
-                        mx(ps, o, n, "w1", g, m, xq[i % 2][:, g], xs[i % 2][:, g], lo + o, g == 0, g == 1)
-                w = sum(n for o, n in pieces)
-                nc.scalar.activation(
-                    out=vis[i][:, m, lo : lo + w], in_=ps[:, :w], func=FUNC.Tanh, bias=l1b[:, m : m + 1]
-                )
+            ps = ps1.tile([P, 512], F32, name="ps", tag="ps1")
+            for o, n in pieces:
+                for g in range(2):
+                    mx(ps, o, n, "w1", g, m, xq[i % 2][:, g], xs[i % 2][:, g], lo + o, g == 0, g == 1)
+            nc.scalar.activation(out=vis[i][:, m, lo : lo + w], in_=ps[:, :w], func=FUNC.Tanh, bias=l1b[:, m : m + 1])
 
-        def v(i):
-            nc.vector.tensor_copy(out=vg[:], in_=vis[i][:].rearrange("p m c -> p c m"))
+        def v(j):
+            i, h = divmod(j, 2)
+            lo, w, pieces = HALVES[h]
+            nc.vector.tensor_copy(out=vg[h][:, :w, :], in_=vis[i][:, :, lo : lo + w].rearrange("p m c -> p c m"))
 
-        def qv(i):
-            quant(vc[i % 2], vs[i % 2], vg)
+        def qv(j):
+            h = j % 2
+            quant(vc[h], vs[h], vg[h], HALVES[h][2])
 
-        def mm2(i, m):
-            if m == 0:
+        def mm2(j, m):
+            i, h = divmod(j, 2)
+            lo, w, pieces = HALVES[h]
+            if h == 0 and m == 0:
                 es[i] = late.tile([P, NCH, COLS], F32, name="e")
-            for lo, pieces in ((0, ((0, 512),)), (512, ((0, 256), (256, 128)))):
-                ps = ps2.tile([P, 512], F32, name="pz", tag="ps2")
-                for o, n in pieces:
-                    mx(ps, o, n, "w2", 0, m, vc[i % 2], vs[i % 2], lo + o, True, False)
-                    for q in range(o, o + n, P):
-                        mx(ps, q, P, "w3", 0, m, uq, us, i * P, False, q + P == o + n)
-                w = sum(n for o, n in pieces)
-                nc.scalar.activation(
-                    out=es[i][:, m, lo : lo + w], in_=ps[:, :w], func=FUNC.Tanh, bias=bu[:, m : m + 1]
-                )
+            ps = ps2.tile([P, 512], F32, name="pz", tag="ps2")
+            for o, n in pieces:
+                mx(ps, o, n, "w2", 0, m, vc[h], vs[h], o, True, False)
+                for q in range(o, o + n, P):
+                    mx(ps, q, P, "w3", 0, m, uq, us, i * P, False, q + P == o + n)
+            nc.scalar.activation(out=es[i][:, m, lo : lo + w], in_=ps[:, :w], func=FUNC.Tanh, bias=bu[:, m : m + 1])
 
-        def ex(i, lo, hi):
-            nc.scalar.activation(out=es[i][:, lo:hi, :], in_=es[i][:, lo:hi, :], func=FUNC.Exp)
+        def ex(j, m0, m1):
+            i, h = divmod(j, 2)
+            lo, w, pieces = HALVES[h]
+            part = es[i][:, m0:m1, lo : lo + w]
+            nc.scalar.activation(out=part, in_=part, func=FUNC.Exp)
 
-        def prod(i, lo, hi):
-            nc.vector.tensor_tensor(
-                out=vis[i][:, lo:hi, :], in0=es[i][:, lo:hi, :], in1=vis[i][:, lo:hi, :], op=ALU.mult
-            )
+        def prod(j, m0, m1):
+            i, h = divmod(j, 2)
+            lo, w, pieces = HALVES[h]
+            part = vis[i][:, m0:m1, lo : lo + w]
+            nc.vector.tensor_tensor(out=part, in0=es[i][:, m0:m1, lo : lo + w], in1=part, op=ALU.mult)
 
         def tr(i, nd, lo, hi):
             data = es[i] if nd == "den" else vis[i]
@@ -206,11 +211,16 @@ def tile_attentionmechanism_pa_t_kernel(tc, v_i, v_q, l1_w, l1_b, w_vi0, w_u0, b
             )
             nc.vector.tensor_copy(out=tail[nd][:, :, :, i], in_=pbs[nd][:, :, TB * RUN : P])
 
-        def ratio():
-            for nd in ("den", "num"):
-                nc.vector.tensor_reduce(out=sums[nd][:, :, TB * NT : B], in_=tail[nd][:], axis=AXIS.X, op=ALU.add)
-            nc.vector.reciprocal(out=sums["den"][:], in_=sums["den"][:])
-            nc.vector.tensor_tensor(out=sums["num"][:], in0=sums["num"][:], in1=sums["den"][:], op=ALU.mult)
+        def red_tail(nd):
+            nc.vector.tensor_reduce(out=sums[nd][:, :, TB * NT : B], in_=tail[nd][:], axis=AXIS.X, op=ALU.add)
+
+        def recip(lo, hi):
+            nc.vector.reciprocal(out=sums["den"][:, :, lo:hi], in_=sums["den"][:, :, lo:hi])
+
+        def ratio(lo, hi):
+            nc.vector.tensor_tensor(
+                out=sums["num"][:, :, lo:hi], in0=sums["num"][:, :, lo:hi], in1=sums["den"][:, :, lo:hi], op=ALU.mult
+            )
 
         def finish():
             po = ps1.tile([P, NCH, P], F32, name="po", tag="ps1")
@@ -291,7 +301,7 @@ def tile_attentionmechanism_pa_t_kernel(tc, v_i, v_q, l1_w, l1_b, w_vi0, w_u0, b
                 )
 
             def uqu():
-                quant(uq, us, urep[:].rearrange("p n c t -> p (n c) t"))
+                quant(uq, us, urep[:].rearrange("p n c t -> p (n c) t"), ((0, 512), (512, 256), (768, 128)))
 
             loadb()
             loadw("w1")
@@ -308,19 +318,22 @@ def tile_attentionmechanism_pa_t_kernel(tc, v_i, v_q, l1_w, l1_b, w_vi0, w_u0, b
             wq("w1", 0)
             rx(0, 1)
             wq("w1", 1)
-            qx(0)
-            for m in range(NCH):
-                mm1(0, m)
+            qx(0, 0)
+            qx(0, 1)
+            for j in range(2):
+                for m in range(NCH):
+                    mm1(j, m)
             rx(1, 0)
+            v(0)
             rx(1, 1)
+            qv(0)
             for c in range(4):
                 uc(c)
             usc()
             wt("w3", 0)
             wt("w2", 0)
-            v(0)
-            qx(1)
-            qv(0)
+            qx(1, 0)
+            qx(1, 1)
             ugr()
             wq("w3", 0)
             urp()
@@ -328,56 +341,70 @@ def tile_attentionmechanism_pa_t_kernel(tc, v_i, v_q, l1_w, l1_b, w_vi0, w_u0, b
             uqu()
 
         late = ctx.enter_context(tc.tile_pool(name="late", bufs=3))
-        for i in range(NT):
-            if i + 2 < NT:
+        nb = 2 * NT
+        for j in range(nb):
+            i, h = divmod(j, 2)
+            nd = "num" if h else "den"
+            if h == 0 and i + 2 < NT:
                 load(i + 2)
-            if i + 1 < NT:
-                for m in range(NCH):
-                    mm1(i + 1, m)
-            if i >= 1:
-                prod(i - 1, 0, 2)
-                prod(i - 1, 2, 4)
-            if i >= 2:
-                back("den")
+            if j + 1 < nb:
+                v(j + 1)
+            if i + 2 < NT:
+                if h == 0:
+                    rx(i + 2, 0)
+                else:
+                    qx(i + 2, 0)
+            if j + 1 < nb:
+                qv(j + 1)
+            if i + 2 < NT:
+                if h == 0:
+                    rx(i + 2, 1)
+                else:
+                    qx(i + 2, 1)
+            if j >= 1:
+                prod(j - 1, 0, 4)
+            front = j + 2 < nb
+            for m in range(2):
+                if front:
+                    mm1(j + 2, m)
+            if h == 0 and i >= 2:
                 back("num")
-            for m in range(NCH):
-                mm2(i, m)
-            if i + 2 < NT:
-                rx(i + 2, 0)
-            if i + 1 < NT:
-                v(i + 1)
-            if i + 2 < NT:
-                rx(i + 2, 1)
-            if i + 1 < NT:
-                qv(i + 1)
-            if i >= 2:
-                red(i - 2, "den")
                 red(i - 2, "num")
-            if i + 2 < NT:
-                qx(i + 2)
-            ex(i, 0, 2)
+            if h == 1 and i >= 1:
+                back("den")
+                red(i - 1, "den")
             if i >= 1:
-                tr(i - 1, "den", 0, NCH)
-                evac("den")
-            ex(i, 2, 4)
+                tr(i - 1, nd, 0, 2)
+            for m in range(2):
+                if front:
+                    mm1(j + 2, 2 + m)
+                mm2(j, m)
             if i >= 1:
-                tr(i - 1, "num", 0, NCH)
-                evac("num")
+                tr(i - 1, nd, 2, 4)
+            for m in range(2, 4):
+                mm2(j, m)
+            if i >= 1:
+                evac(nd)
+            if j < nb - 1:
+                ex(j, 0, 4)
         last = NT - 1
-        back("den")
         back("num")
-        prod(last, 0, 2)
-        prod(last, 2, 4)
-        red(last - 1, "den")
         red(last - 1, "num")
+        recip(0, TB * last)
+        ratio(0, TB * last)
+        for m in range(NCH):
+            ex(nb - 1, m, m + 1)
+            prod(nb - 1, m, m + 1)
         tr(last, "den", 0, NCH)
+        tr(last, "num", 0, NCH)
         evac("den")
-        tr(last, "num", 0, 2)
-        tr(last, "num", 2, 4)
         evac("num")
         back("den")
-        back("num")
         red(last, "den")
+        red_tail("den")
+        recip(TB * last, B)
+        back("num")
         red(last, "num")
-        ratio()
+        red_tail("num")
+        ratio(TB * last, B)
         finish()

@@ -101,10 +101,12 @@ def tile_attentionmechanism_pa_t_kernel(tc, v_i, v_q, l1_w, l1_b, w_vi0, w_u0, b
 
         def rx(i, g):
             dst = xg[:, g].rearrange("p (k c) t -> p k c t", c=P)
-            nc.vector.tensor_copy(
-                out=dst[:, :, 0 : TB * RUN, :].rearrange("p k (b r) t -> p b k t r", r=RUN),
-                in_=raws[i][g][:].rearrange("p b (t k r) -> p b k t r", t=4, r=RUN),
-            )
+            src = raws[i][g][:].rearrange("p b (t k r) -> p k b t r", t=4, r=RUN)
+            for lo, hi in ((0, KK - 1), (KK - 1, KK)):
+                nc.vector.tensor_copy(
+                    out=dst[:, lo:hi, 0 : TB * RUN, :].rearrange("p k (b r) t -> p k b t r", r=RUN),
+                    in_=src[:, lo:hi],
+                )
             nc.vector.tensor_copy(
                 out=dst[:, :, TB * RUN : P, :].rearrange("p k x t -> p x k t"),
                 in_=rawx[g][:].rearrange("p x (t k r) -> p x k t r", t=4, r=RUN)[:, :, :, :, i],

@@ -19,6 +19,7 @@ NT = 7
 TB = 18
 RUN = 7
 KK = 7
+ROW = 208
 COLS = KK * P
 HALVES = ((0, 512, ((0, 512),)), (512, 384, ((0, 256), (256, 128))))
 FLOPS = 2 * B * S * C * HID + 2 * B * S * HID * HID + 2 * B * HID * HID
@@ -43,7 +44,7 @@ def tile_attentionmechanism_pa_t_kernel(tc, v_i, v_q, l1_w, l1_b, w_vi0, w_u0, b
         vg = [keep.tile([P, 512, 4], BF16, align_bytes=64, name="vg%d" % i) for i in range(2)]
         vc = [keep.tile([P, 512], U32, align_bytes=64, name="vc%d" % i) for i in range(2)]
         vs = [keep.tile([P, 512], U8, align_bytes=64, name="vs%d" % i) for i in range(2)]
-        rawx = [keep.tile([P, 2, 4 * S], BF16, name="rawx%d" % g) for g in range(2)]
+        rawx = [keep.tile([P, 2, ROW], BF16, name="rawx%d" % g) for g in range(2)]
 
         ident32 = keep.tile([P, P], F32, name="ident32")
         make_identity(nc, ident32[:])
@@ -77,17 +78,17 @@ def tile_attentionmechanism_pa_t_kernel(tc, v_i, v_q, l1_w, l1_b, w_vi0, w_u0, b
         pst_u = {}
 
         def load(i):
-            raws[i] = [rawp.tile([P, TB, 4 * S], BF16, name="raw%d" % g) for g in range(2)]
+            raws[i] = [rawp.tile([P, TB, ROW], BF16, name="raw%d" % g) for g in range(2)]
             for g in range(2):
                 nc.sync.dma_start(
-                    out=raws[i][g][:],
+                    out=raws[i][g][:, :, : 4 * S],
                     in_=v_i[TB * i : TB * (i + 1), g * 512 : (g + 1) * 512].rearrange("b (p t) h w -> p b (t h w)", t=4),
                 )
 
         def loadx():
             for g in range(2):
                 nc.sync.dma_start(
-                    out=rawx[g][:],
+                    out=rawx[g][:, :, : 4 * S],
                     in_=v_i[TB * NT : B, g * 512 : (g + 1) * 512].rearrange("b (p t) h w -> p b (t h w)", t=4),
                 )
 
@@ -101,7 +102,7 @@ def tile_attentionmechanism_pa_t_kernel(tc, v_i, v_q, l1_w, l1_b, w_vi0, w_u0, b
 
         def rx(i, g):
             dst = xg[:, g].rearrange("p (k c) t -> p k c t", c=P)
-            src = raws[i][g][:].rearrange("p b (t k r) -> p k b t r", t=4, r=RUN)
+            src = raws[i][g][:, :, : 4 * S].rearrange("p b (t k r) -> p k b t r", t=4, r=RUN)
             for lo, hi in ((0, KK - 1), (KK - 1, KK)):
                 nc.vector.tensor_copy(
                     out=dst[:, lo:hi, 0 : TB * RUN, :].rearrange("p k (b r) t -> p k b t r", r=RUN),
@@ -109,7 +110,7 @@ def tile_attentionmechanism_pa_t_kernel(tc, v_i, v_q, l1_w, l1_b, w_vi0, w_u0, b
                 )
             nc.vector.tensor_copy(
                 out=dst[:, :, TB * RUN : P, :].rearrange("p k x t -> p x k t"),
-                in_=rawx[g][:].rearrange("p x (t k r) -> p x k t r", t=4, r=RUN)[:, :, :, :, i],
+                in_=rawx[g][:, :, : 4 * S].rearrange("p x (t k r) -> p x k t r", t=4, r=RUN)[:, :, :, :, i],
             )
 
         def quant(codes, scales, src, pieces):

@@ -143,9 +143,9 @@ def tile_attentionmechanism_pa_t_kernel(tc, v_i, v_q, l1_w, l1_b, w_vi0, w_u0, b
             if h == 0 and m == 0:
                 vis[i] = vip.tile([P, NCH, COLS], F32, name="vi")
             ps = ps1.tile([P, 512], F32, name="ps", tag="ps1")
-            for o, n in pieces:
-                for g in range(2):
-                    mx(ps, o, n, "w1", g, m, xq[i % 2][:, g], xs[i % 2][:, g], lo + o, g == 0, g == 1)
+            for g in range(2):
+                for o, n in pieces:
+                    mx(ps, o, n, "w1", g, m, xq[i % 2][:, g], xs[i % 2][:, g], lo + o, g == 0 and o == 0, g == 1 and o + n == w)
             nc.scalar.activation(out=vis[i][:, m, lo : lo + w], in_=ps[:, :w], func=FUNC.Tanh, bias=l1b[:, m : m + 1])
 
         def v(j):
@@ -164,9 +164,9 @@ def tile_attentionmechanism_pa_t_kernel(tc, v_i, v_q, l1_w, l1_b, w_vi0, w_u0, b
                 es[i] = late.tile([P, NCH, COLS], F32, name="e")
             ps = ps2.tile([P, 512], F32, name="pz", tag="ps2")
             for o, n in pieces:
-                mx(ps, o, n, "w2", 0, m, vc[h], vs[h], o, True, False)
-                for q in range(o, o + n, P):
-                    mx(ps, q, P, "w3", 0, m, uq, us, i * P, False, q + P == o + n)
+                mx(ps, o, n, "w2", 0, m, vc[h], vs[h], o, o == 0, False)
+            for q in range(0, w, P):
+                mx(ps, q, P, "w3", 0, m, uq, us, i * P, False, q + P == w)
             nc.scalar.activation(out=es[i][:, m, lo : lo + w], in_=ps[:, :w], func=FUNC.Tanh, bias=bu[:, m : m + 1])
 
         def ex(j, m0, m1):
@@ -185,15 +185,15 @@ def tile_attentionmechanism_pa_t_kernel(tc, v_i, v_q, l1_w, l1_b, w_vi0, w_u0, b
             data = es[i] if nd == "den" else vis[i]
             if lo == 0:
                 pts[nd] = pst.tile([P, NCH, P], F32, name="pt", tag="pst")
-            for m in range(lo, hi):
-                for k in range(KK):
+            for k in range(lo, hi):
+                for m in range(NCH):
                     nc.tensor.matmul(
                         pts[nd][:, m, :],
                         lhsT=data[:, m, k * P : (k + 1) * P],
                         rhs=ident32[:],
                         is_transpose=True,
-                        start=(k == 0),
-                        stop=(k == KK - 1),
+                        start=(k == 0 and m == 0),
+                        stop=(k == KK - 1 and m == NCH - 1),
                     )
 
         def evac(nd):
@@ -377,13 +377,13 @@ def tile_attentionmechanism_pa_t_kernel(tc, v_i, v_q, l1_w, l1_b, w_vi0, w_u0, b
                 back("den")
                 red(i - 1, "den")
             if i >= 1:
-                tr(i - 1, nd, 0, 2)
+                tr(i - 1, nd, 0, 4)
             for m in range(2):
                 if front:
                     mm1(j + 2, 2 + m)
                 mm2(j, m)
             if i >= 1:
-                tr(i - 1, nd, 2, 4)
+                tr(i - 1, nd, 4, KK)
             for m in range(2, 4):
                 mm2(j, m)
             if i >= 1:
@@ -398,8 +398,8 @@ def tile_attentionmechanism_pa_t_kernel(tc, v_i, v_q, l1_w, l1_b, w_vi0, w_u0, b
         for m in range(NCH):
             ex(nb - 1, m, m + 1)
             prod(nb - 1, m, m + 1)
-        tr(last, "den", 0, NCH)
-        tr(last, "num", 0, NCH)
+        tr(last, "den", 0, KK)
+        tr(last, "num", 0, KK)
         evac("den")
         evac("num")
         back("den")

@@ -19,7 +19,9 @@ NT = 7
 TB = 18
 RUN = 7
 KK = 7
-ROW = 208
+WIN = 256
+OFF = WIN - 4 * S
+ROW = OFF + WIN + 4
 COLS = KK * P
 HALVES = ((0, 512, ((0, 512),)), (512, 384, ((0, 256), (256, 128))))
 FLOPS = 2 * B * S * C * HID + 2 * B * S * HID * HID + 2 * B * HID * HID
@@ -77,20 +79,19 @@ def tile_attentionmechanism_pa_t_kernel(tc, v_i, v_q, l1_w, l1_b, w_vi0, w_u0, b
         pbs = {}
         pst_u = {}
 
+        def loadrows(raw, b0, b1, g):
+            pairs = v_i[b0:b1, g * 512 : (g + 1) * 512].rearrange("b (p t) h w -> p b (t h w)", t=8)
+            nc.sync.dma_start(out=raw[0:P:2, :, OFF : OFF + WIN], in_=pairs[:, :, 0:WIN])
+            nc.sync.dma_start(out=raw[1:P:2, :, 0:WIN], in_=pairs[:, :, 8 * S - WIN : 8 * S])
+
         def load(i):
             raws[i] = [rawp.tile([P, TB, ROW], BF16, name="raw%d" % g) for g in range(2)]
             for g in range(2):
-                nc.sync.dma_start(
-                    out=raws[i][g][:, :, : 4 * S],
-                    in_=v_i[TB * i : TB * (i + 1), g * 512 : (g + 1) * 512].rearrange("b (p t) h w -> p b (t h w)", t=4),
-                )
+                loadrows(raws[i][g], TB * i, TB * (i + 1), g)
 
         def loadx():
             for g in range(2):
-                nc.sync.dma_start(
-                    out=rawx[g][:, :, : 4 * S],
-                    in_=v_i[TB * NT : B, g * 512 : (g + 1) * 512].rearrange("b (p t) h w -> p b (t h w)", t=4),
-                )
+                loadrows(rawx[g], TB * NT, B, g)
 
         def loadb():
             nc.scalar.dma_start(out=l1b_raw[:], in_=l1_b.rearrange("(j m) -> j m", m=NCH))
@@ -100,17 +101,23 @@ def tile_attentionmechanism_pa_t_kernel(tc, v_i, v_q, l1_w, l1_b, w_vi0, w_u0, b
             nc.vector.tensor_copy(out=l1b[:], in_=l1b_raw[:])
             nc.vector.tensor_copy(out=bu[:], in_=bu_raw[:])
 
-        def rx(i, g):
+        def rx_scalar(i, g, ks):
             dst = xg[:, g].rearrange("p (k c) t -> p k c t", c=P)
-            src = raws[i][g][:, :, : 4 * S].rearrange("p b (t k r) -> p k b t r", t=4, r=RUN)
-            for lo, hi in ((0, KK - 1), (KK - 1, KK)):
+            src = raws[i][g][:, :, OFF:WIN].rearrange("p b (t k r) -> p k b r t", t=4, r=RUN)
+            for k in ks:
+                nc.scalar.copy(out=dst[:, k, 0 : TB * RUN, :].rearrange("p (b r) t -> p b r t", r=RUN), in_=src[:, k])
+
+        def rx(i, g, ks=((0, KK - 1), (KK - 1, KK))):
+            dst = xg[:, g].rearrange("p (k c) t -> p k c t", c=P)
+            src = raws[i][g][:, :, OFF:WIN].rearrange("p b (t k r) -> p k b t r", t=4, r=RUN)
+            for lo, hi in ks:
                 nc.vector.tensor_copy(
                     out=dst[:, lo:hi, 0 : TB * RUN, :].rearrange("p k (b r) t -> p k b t r", r=RUN),
                     in_=src[:, lo:hi],
                 )
             nc.vector.tensor_copy(
                 out=dst[:, :, TB * RUN : P, :].rearrange("p k x t -> p x k t"),
-                in_=rawx[g][:, :, : 4 * S].rearrange("p x (t k r) -> p x k t r", t=4, r=RUN)[:, :, :, :, i],
+                in_=rawx[g][:, :, OFF:WIN].rearrange("p x (t k r) -> p x k t r", t=4, r=RUN)[:, :, :, :, i],
             )
 
         def quant(codes, scales, src, pieces):
@@ -121,10 +128,9 @@ def tile_attentionmechanism_pa_t_kernel(tc, v_i, v_q, l1_w, l1_b, w_vi0, w_u0, b
                     in_=src[:, o : o + n, :].rearrange("p c t -> p (c t)"),
                 )
 
-        def qx(i, h):
+        def qx(i, h, g):
             lo, w, pieces = HALVES[h]
-            for g in range(2):
-                quant(xq[i % 2][:, g, lo : lo + w], xs[i % 2][:, g, lo : lo + w], xg[:, g, lo : lo + w, :], pieces)
+            quant(xq[i % 2][:, g, lo : lo + w], xs[i % 2][:, g, lo : lo + w], xg[:, g, lo : lo + w, :], pieces)
 
         def mx(ps, o, n, w, g, m, codes, scales, c, start, stop):
             nc.tensor.matmul_mx(
@@ -183,8 +189,10 @@ def tile_attentionmechanism_pa_t_kernel(tc, v_i, v_q, l1_w, l1_b, w_vi0, w_u0, b
 
         def tr(i, nd, lo, hi):
             data = es[i] if nd == "den" else vis[i]
-            if lo == 0:
+            if lo == 0 and i < NT - 1:
                 pts[nd] = pst.tile([P, NCH, P], F32, name="pt", tag="pst")
+            elif lo == 0:
+                pts[nd] = ps1.tile([P, NCH, P], F32, name="pt", tag="ps1")
             for k in range(lo, hi):
                 for m in range(NCH):
                     nc.tensor.matmul(
@@ -196,9 +204,9 @@ def tile_attentionmechanism_pa_t_kernel(tc, v_i, v_q, l1_w, l1_b, w_vi0, w_u0, b
                         stop=(k == KK - 1 and m == NCH - 1),
                     )
 
-        def evac(nd):
+        def evac(nd, copy=nc.scalar.copy):
             sjs[nd] = sjp.tile([P, NCH, P], F32, name="sj_" + nd)
-            nc.scalar.copy(out=sjs[nd][:], in_=pts[nd][:])
+            copy(out=sjs[nd][:], in_=pts[nd][:])
 
         def back(nd):
             pbs[nd] = pst.tile([P, NCH, P], F32, name="pb", tag="pst")
@@ -290,123 +298,146 @@ def tile_attentionmechanism_pa_t_kernel(tc, v_i, v_q, l1_w, l1_b, w_vi0, w_u0, b
             def ugr():
                 nc.vector.tensor_copy(out=ug[:], in_=pst_u["put"][:].rearrange("j m b -> j b m"))
 
-            def urp():
+            def uqu(lo, hi, pieces):
+                n = hi - lo
                 nc.vector.tensor_copy(
-                    out=urep[:, :, 0 : TB * RUN, :].rearrange("p n (b r) t -> p n b r t", r=RUN),
-                    in_=ug[:, 0 : TB * NT, :]
-                    .rearrange("p (n b) t -> p n b t", n=NT)
+                    out=urep[:, lo:hi, 0 : TB * RUN, :].rearrange("p n (b r) t -> p n b r t", r=RUN),
+                    in_=ug[:, TB * lo : TB * hi, :]
+                    .rearrange("p (n b) t -> p n b t", n=n)
                     .unsqueeze(3)
-                    .to_broadcast([P, NT, TB, RUN, 4]),
+                    .to_broadcast([P, n, TB, RUN, 4]),
                 )
                 nc.vector.tensor_copy(
-                    out=urep[:, :, TB * RUN : P, :],
-                    in_=ug[:, TB * NT : B, :].unsqueeze(1).to_broadcast([P, NT, 2, 4]),
+                    out=urep[:, lo:hi, TB * RUN : P, :],
+                    in_=ug[:, TB * NT : B, :].unsqueeze(1).to_broadcast([P, n, 2, 4]),
                 )
-
-            def uqu():
-                quant(uq, us, urep[:].rearrange("p n c t -> p (n c) t"), ((0, 512), (512, 256), (768, 128)))
+                quant(
+                    uq[:, lo * P : hi * P], us[:, lo * P : hi * P], urep[:, lo:hi].rearrange("p n c t -> p (n c) t"), pieces
+                )
 
             loadb()
             loadw("w1")
             loadx()
             load(0)
-            load(1)
-            loadvq()
             loadw("w3")
             loadw("w2")
+            load(1)
+            loadvq()
             castb()
             wt("w1", 0)
             wt("w1", 1)
             rx(0, 0)
             wq("w1", 0)
-            rx(0, 1)
             wq("w1", 1)
-            qx(0, 0)
-            qx(0, 1)
+            qx(0, 0, 0)
+            qx(0, 1, 0)
+            rx_scalar(0, 1, range(4, KK))
+            rx(0, 1, ((0, 4),))
+            wt("w3", 0)
+            wt("w2", 0)
+            qx(0, 0, 1)
+            qx(0, 1, 1)
             for j in range(2):
                 for m in range(NCH):
                     mm1(j, m)
             rx(1, 0)
             v(0)
-            rx(1, 1)
             qv(0)
+            v(1)
+            qv(1)
+            qx(1, 0, 0)
+            qx(1, 1, 0)
+            rx_scalar(1, 1, range(KK))
+            rx(1, 1, ())
+            wq("w3", 0)
+            wq("w2", 0)
             for c in range(4):
                 uc(c)
             usc()
-            wt("w3", 0)
-            wt("w2", 0)
-            qx(1, 0)
-            qx(1, 1)
             ugr()
-            wq("w3", 0)
-            urp()
-            wq("w2", 0)
-            uqu()
+            qx(1, 0, 1)
+            uqu(0, 1, ((0, 128),))
+            qx(1, 1, 1)
+            uqu(1, NT, ((0, 512), (512, 256)))
 
         late = ctx.enter_context(tc.tile_pool(name="late", bufs=3))
         nb = 2 * NT
+        last = NT - 1
         for j in range(nb):
             i, h = divmod(j, 2)
             nd = "num" if h else "den"
+            other = "den" if h else "num"
+            front = j + 2 < nb
             if h == 0 and i + 2 < NT:
                 load(i + 2)
-            if j + 1 < nb:
+            if 0 < j < nb - 1:
                 v(j + 1)
             if i + 2 < NT:
                 if h == 0:
                     rx(i + 2, 0)
                 else:
-                    qx(i + 2, 0)
-            if j + 1 < nb:
+                    qx(i + 2, 0, 0)
+                    qx(i + 2, 0, 1)
+            if 0 < j < nb - 1:
                 qv(j + 1)
             if i + 2 < NT:
                 if h == 0:
                     rx(i + 2, 1)
                 else:
-                    qx(i + 2, 1)
+                    qx(i + 2, 1, 0)
+                    qx(i + 2, 1, 1)
+            if nb - 4 <= j < nb - 2:
+                recip(2 * TB * (j - nb + 4), 2 * TB * (j - nb + 5))
+            if j == nb - 2:
+                recip(TB * (last - 2), TB * (last - 1))
             if j >= 1:
                 prod(j - 1, 0, 4)
-            front = j + 2 < nb
-            for m in range(2):
-                if front:
-                    mm1(j + 2, m)
-            if h == 0 and i >= 2:
-                back("num")
-                red(i - 2, "num")
-            if h == 1 and i >= 1:
-                back("den")
-                red(i - 1, "den")
-            if i >= 1:
-                tr(i - 1, nd, 0, 4)
-            for m in range(2):
-                if front:
+            if front:
+                mm1(j + 2, 0)
+                mm1(j + 2, 1)
+                if i >= 1:
+                    tr(i - 1, nd, 0, 4)
+                for m in range(2):
                     mm1(j + 2, 2 + m)
-                mm2(j, m)
+                    mm2(j, m)
+            else:
+                for m in range(NCH):
+                    mm2(j, m)
+                if j < nb - 1:
+                    ex(j, 0, 4)
+                tr(i - 1, nd, 0, 4)
+            if i >= 1 + (1 - h):
+                back(other)
+                red(i - 2 + h, other)
             if i >= 1:
                 tr(i - 1, nd, 4, KK)
-            for m in range(2, 4):
-                mm2(j, m)
-            if i >= 1:
-                evac(nd)
-            if j < nb - 1:
+            if front:
+                for m in range(2, 4):
+                    mm2(j, m)
+                if i >= 1:
+                    evac(nd)
                 ex(j, 0, 4)
-        last = NT - 1
-        back("num")
-        red(last - 1, "num")
-        recip(0, TB * last)
-        ratio(0, TB * last)
+            elif j < nb - 1:
+                evac(nd, nc.vector.tensor_copy)
+        recip(TB * (last - 1), TB * last)
+        evac("num", nc.vector.tensor_copy)
         for m in range(NCH):
             ex(nb - 1, m, m + 1)
             prod(nb - 1, m, m + 1)
-        tr(last, "den", 0, KK)
-        tr(last, "num", 0, KK)
+        tr(last, "den", 0, 4)
+        back("num")
+        red(last - 1, "num")
+        tr(last, "num", 0, 4)
+        tr(last, "den", 4, KK)
         evac("den")
-        evac("num")
+        tr(last, "num", 4, KK)
+        evac("num", nc.vector.tensor_copy)
         back("den")
+        back("num")
+        ratio(0, TB * last)
         red(last, "den")
         red_tail("den")
         recip(TB * last, B)
-        back("num")
         red(last, "num")
         red_tail("num")
         ratio(TB * last, B)

@@ -6,6 +6,7 @@ from concourse.masks import make_identity
 F32 = mybir.dt.float32
 BF16 = mybir.dt.bfloat16
 U32 = mybir.dt.uint32
+I32 = mybir.dt.int32
 U8 = mybir.dt.uint8
 FP8X4 = mybir.dt.float8_e4m3fn_x4
 FUNC = mybir.ActivationFunctionType
@@ -15,38 +16,35 @@ AXIS = mybir.AxisListType
 B, C, S, T, HID = 128, 1024, 49, 20, 512
 P = 128
 NCH = 4
-NT = 7
-TB = 18
-RUN = 7
-KK = 7
-WIN = 256
-OFF = WIN - 4 * S
-ROW = OFF + WIN + 4
-COLS = KK * P
-HALVES = ((0, 512, ((0, 512),)), (512, 384, ((0, 256), (256, 128))))
+W = 512
+ROW = 208
+CH = 16
+TILES = ((0, 16), (16, 16), (32, 32), (64, 32), (96, 32))
+STEPS = (
+    [(t, k, n) for t in (0, 1) for k, n in ((0, 4), (4, 2))]
+    + [(t, k, 4) for t in (2, 3) for k in (0, 4, 8)]
+    + [(4, 0, 4), (None, 0, 1), (4, 4, 4), (4, 8, 4)]
+)
 FLOPS = 2 * B * S * C * HID + 2 * B * S * HID * HID + 2 * B * HID * HID
 
 
 def tile_attentionmechanism_pa_t_kernel(tc, v_i, v_q, l1_w, l1_b, w_vi0, w_u0, b_u0, out):
     nc = tc.nc
+    ns = len(STEPS)
+    jl = STEPS.index((None, 0, 1))
 
     with ExitStack() as ctx:
         keep = ctx.enter_context(tc.tile_pool(name="keep", bufs=1))
-        rawp = ctx.enter_context(tc.tile_pool(name="rawp", bufs=2))
-        vip = ctx.enter_context(tc.tile_pool(name="vip", bufs=3))
-        sjp = ctx.enter_context(tc.tile_pool(name="sjp", bufs=2))
+        rawp = ctx.enter_context(tc.tile_pool(name="rawp", bufs=4))
+        xgp = ctx.enter_context(tc.tile_pool(name="xgp", bufs=3))
+        two = ctx.enter_context(tc.tile_pool(name="two", bufs=2))
+        vip = ctx.enter_context(tc.tile_pool(name="vip", bufs=5))
         ps1 = ctx.enter_context(tc.psum_pool(name="ps1", bufs=3))
         ps2 = ctx.enter_context(tc.psum_pool(name="ps2", bufs=3))
-        pst = ctx.enter_context(tc.psum_pool(name="pst", bufs=2))
+        pst = ctx.enter_context(tc.psum_pool(name="pst", bufs=1))
         ctx.enter_context(tc.manual_schedule())
 
-        xg = keep.tile([P, 2, COLS, 4], BF16, align_bytes=64, name="xg")
-        xq = [keep.tile([P, 2, COLS], U32, align_bytes=64, name="xq%d" % i) for i in range(2)]
-        xs = [keep.tile([P, 2, COLS], U8, align_bytes=64, name="xs%d" % i) for i in range(2)]
-        vg = [keep.tile([P, 512, 4], BF16, align_bytes=64, name="vg%d" % i) for i in range(2)]
-        vc = [keep.tile([P, 512], U32, align_bytes=64, name="vc%d" % i) for i in range(2)]
-        vs = [keep.tile([P, 512], U8, align_bytes=64, name="vs%d" % i) for i in range(2)]
-        rawx = [keep.tile([P, 2, ROW], BF16, name="rawx%d" % g) for g in range(2)]
+        xl = keep.tile([P, 2, P, 4], BF16, align_bytes=64, name="xl")
 
         ident32 = keep.tile([P, P], F32, name="ident32")
         make_identity(nc, ident32[:])
@@ -65,13 +63,21 @@ def tile_attentionmechanism_pa_t_kernel(tc, v_i, v_q, l1_w, l1_b, w_vi0, w_u0, b
         l1b = keep.tile([P, NCH], F32, name="l1b")
         bu = keep.tile([P, NCH], F32, name="bu")
         u32 = keep.tile([P, NCH, P], F32, name="u32")
-        uq = keep.tile([P, NT * P], U32, align_bytes=64, name="uq")
-        us = keep.tile([P, NT * P], U8, align_bytes=64, name="us")
+        uq = {t: keep.tile([P, 4, P], U32, align_bytes=64, name="uq%d" % t) for t in range(len(TILES))}
+        us = {t: keep.tile([P, 4, P], U8, align_bytes=64, name="us%d" % t) for t in range(len(TILES))}
+        uq[None] = keep.tile([P, 1, P], U32, align_bytes=64, name="uql")
+        us[None] = keep.tile([P, 1, P], U8, align_bytes=64, name="usl")
         sums = {nd: keep.tile([P, NCH, B], F32, name="sum_" + nd) for nd in ("num", "den")}
-        tail = {nd: keep.tile([P, NCH, 2, NT], F32, name="tail_" + nd) for nd in ("num", "den")}
+        sj = {nd: keep.tile([P, NCH, P], F32, name="sj_" + nd) for nd in ("num", "den")}
         osb = keep.tile([P, P, NCH], F32, name="osb")
+        for t in range(len(TILES)):
+            nc.gpsimd.memset(us[t][:, 0, :].bitcast(I32), 0)
 
         raws = {}
+        xgs = {}
+        xqs = {}
+        vgs = {}
+        vcs = {}
         vis = {}
         es = {}
         pts = {}
@@ -79,151 +85,157 @@ def tile_attentionmechanism_pa_t_kernel(tc, v_i, v_q, l1_w, l1_b, w_vi0, w_u0, b
         pbs = {}
         pst_u = {}
 
-        def loadrows(raw, b0, b1, g):
-            pairs = v_i[b0:b1, g * 512 : (g + 1) * 512].rearrange("b (p t) h w -> p b (t h w)", t=8)
-            nc.sync.dma_start(out=raw[0:P:2, :, OFF : OFF + WIN], in_=pairs[:, :, 0:WIN])
-            nc.sync.dma_start(out=raw[1:P:2, :, 0:WIN], in_=pairs[:, :, 8 * S - WIN : 8 * S])
+        def width(j):
+            return STEPS[j][2] * P
 
-        def load(i):
-            raws[i] = [rawp.tile([P, TB, ROW], BF16, name="raw%d" % g) for g in range(2)]
+        def load(c):
+            raws[c] = [rawp.tile([P, CH, ROW], BF16, name="raw%d" % g) for g in range(2)]
             for g in range(2):
-                loadrows(raws[i][g], TB * i, TB * (i + 1), g)
-
-        def loadx():
-            for g in range(2):
-                loadrows(rawx[g], TB * NT, B, g)
+                nc.sync.dma_start(
+                    out=raws[c][g][:, :, : 4 * S],
+                    in_=v_i[CH * c : CH * (c + 1), g * 512 : (g + 1) * 512].rearrange("b (p t) h w -> p b (t h w)", t=4),
+                )
 
         def loadb():
             nc.scalar.dma_start(out=l1b_raw[:], in_=l1_b.rearrange("(j m) -> j m", m=NCH))
             nc.scalar.dma_start(out=bu_raw[:], in_=b_u0.rearrange("(j m) -> j m", m=NCH))
 
-        def castb():
-            nc.vector.tensor_copy(out=l1b[:], in_=l1b_raw[:])
-            nc.vector.tensor_copy(out=bu[:], in_=bu_raw[:])
+        def castb(dst, src):
+            nc.vector.tensor_copy(out=dst[:], in_=src[:])
 
-        def rx_scalar(i, g, ks):
-            dst = xg[:, g].rearrange("p (k c) t -> p k c t", c=P)
-            src = raws[i][g][:, :, OFF:WIN].rearrange("p b (t k r) -> p k b r t", t=4, r=RUN)
-            for k in ks:
-                nc.scalar.copy(out=dst[:, k, 0 : TB * RUN, :].rearrange("p (b r) t -> p b r t", r=RUN), in_=src[:, k])
-
-        def rx(i, g, ks=((0, KK - 1), (KK - 1, KK))):
-            dst = xg[:, g].rearrange("p (k c) t -> p k c t", c=P)
-            src = raws[i][g][:, :, OFF:WIN].rearrange("p b (t k r) -> p k b t r", t=4, r=RUN)
-            for lo, hi in ks:
+        def rx(j, g):
+            t, k0, nk = STEPS[j]
+            b0, nb = TILES[t]
+            r = P // nb
+            if g == 0:
+                xgs[j] = xgp.tile([P, 2, W, 4], BF16, align_bytes=64, name="xg")
+            dst = xgs[j][:, g, : nk * P, :].rearrange("p (k b r) t -> p k b t r", k=nk, r=r)
+            for c in range(b0 // CH, (b0 + nb) // CH):
+                src = raws[c][g][:, :, : 4 * S].rearrange("p b (t s) -> p b t s", t=4)
                 nc.vector.tensor_copy(
-                    out=dst[:, lo:hi, 0 : TB * RUN, :].rearrange("p k (b r) t -> p k b t r", r=RUN),
-                    in_=src[:, lo:hi],
+                    out=dst[:, :, c * CH - b0 : (c + 1) * CH - b0],
+                    in_=src[:, :, :, k0 * r : (k0 + nk) * r].rearrange("p b t (k r) -> p k b t r", r=r),
                 )
-            nc.vector.tensor_copy(
-                out=dst[:, :, TB * RUN : P, :].rearrange("p k x t -> p x k t"),
-                in_=rawx[g][:, :, OFF:WIN].rearrange("p x (t k r) -> p x k t r", t=4, r=RUN)[:, :, :, :, i],
+                if k0 == 0:
+                    nc.vector.tensor_copy(out=xl[:, g, CH * c : CH * (c + 1), :], in_=src[:, :, :, S - 1])
+
+        def quant(codes, scales, src):
+            nc.vector.quantize_mx(out=codes.bitcast(FP8X4), scales=scales, in_=src)
+
+        def qx(j):
+            w = width(j)
+            xqs[j] = (
+                two.tile([P, 2, W], U32, align_bytes=64, name="xq"),
+                two.tile([P, 2, W], U8, align_bytes=64, name="xs"),
             )
-
-        def quant(codes, scales, src, pieces):
-            for o, n in pieces:
-                nc.vector.quantize_mx(
-                    out=codes[:, o : o + n].bitcast(FP8X4),
-                    scales=scales[:, o : o + n],
-                    in_=src[:, o : o + n, :].rearrange("p c t -> p (c t)"),
+            src = xl if STEPS[j][0] is None else xgs[j]
+            if w == W:
+                quant(
+                    xqs[j][0][:].rearrange("p g c -> p (g c)"),
+                    xqs[j][1][:].rearrange("p g c -> p (g c)"),
+                    src[:].rearrange("p g c t -> p (g c t)"),
                 )
+            else:
+                for g in range(2):
+                    quant(xqs[j][0][:, g, :w], xqs[j][1][:, g, :w], src[:, g, :w, :].rearrange("p c t -> p (c t)"))
 
-        def qx(i, h, g):
-            lo, w, pieces = HALVES[h]
-            quant(xq[i % 2][:, g, lo : lo + w], xs[i % 2][:, g, lo : lo + w], xg[:, g, lo : lo + w, :], pieces)
-
-        def mx(ps, o, n, w, g, m, codes, scales, c, start, stop):
+        def mx(ps, n, w, g, m, codes, scales, start, stop):
             nc.tensor.matmul_mx(
-                out=ps[:, o : o + n],
+                out=ps[:, :n],
                 lhsT=wq_[w][:, g, m * P : (m + 1) * P].bitcast(FP8X4),
                 lhsT_scale=ws_[w][:, g, m * P : (m + 1) * P],
-                rhs=codes[:, c : c + n].bitcast(FP8X4),
-                rhs_scale=scales[:, c : c + n],
+                rhs=codes[:, :n].bitcast(FP8X4),
+                rhs_scale=scales[:, :n],
                 start=start,
                 stop=stop,
             )
 
         def mm1(j, m):
-            i, h = divmod(j, 2)
-            lo, w, pieces = HALVES[h]
-            if h == 0 and m == 0:
-                vis[i] = vip.tile([P, NCH, COLS], F32, name="vi")
-            ps = ps1.tile([P, 512], F32, name="ps", tag="ps1")
+            w = width(j)
+            if m == 0:
+                vis[j] = vip.tile([P, NCH, W], F32, name="vi")
+            ps = ps1.tile([P, W], F32, name="ps", tag="ps1")
             for g in range(2):
-                for o, n in pieces:
-                    mx(ps, o, n, "w1", g, m, xq[i % 2][:, g], xs[i % 2][:, g], lo + o, g == 0 and o == 0, g == 1 and o + n == w)
-            nc.scalar.activation(out=vis[i][:, m, lo : lo + w], in_=ps[:, :w], func=FUNC.Tanh, bias=l1b[:, m : m + 1])
+                mx(ps, w, "w1", g, m, xqs[j][0][:, g], xqs[j][1][:, g], g == 0, g == 1)
+            nc.scalar.activation(out=vis[j][:, m, :w], in_=ps[:, :w], func=FUNC.Tanh, bias=l1b[:, m : m + 1])
 
         def v(j):
-            i, h = divmod(j, 2)
-            lo, w, pieces = HALVES[h]
-            nc.vector.tensor_copy(out=vg[h][:, :w, :], in_=vis[i][:, :, lo : lo + w].rearrange("p m c -> p c m"))
+            w = width(j)
+            vgs[j] = two.tile([P, W, 4], BF16, align_bytes=64, name="vg")
+            nc.vector.tensor_copy(out=vgs[j][:, :w, :], in_=vis[j][:, :, :w].rearrange("p m c -> p c m"))
 
         def qv(j):
-            h = j % 2
-            quant(vc[h], vs[h], vg[h], HALVES[h][2])
+            w = width(j)
+            vcs[j] = (
+                two.tile([P, W], U32, align_bytes=64, name="vc"),
+                two.tile([P, W], U8, align_bytes=64, name="vs"),
+            )
+            quant(vcs[j][0][:, :w], vcs[j][1][:, :w], vgs[j][:, :w, :].rearrange("p c t -> p (c t)"))
 
         def mm2(j, m):
-            i, h = divmod(j, 2)
-            lo, w, pieces = HALVES[h]
-            if h == 0 and m == 0:
-                es[i] = late.tile([P, NCH, COLS], F32, name="e")
-            ps = ps2.tile([P, 512], F32, name="pz", tag="ps2")
-            for o, n in pieces:
-                mx(ps, o, n, "w2", 0, m, vc[h], vs[h], o, o == 0, False)
-            for q in range(0, w, P):
-                mx(ps, q, P, "w3", 0, m, uq, us, i * P, False, q + P == w)
-            nc.scalar.activation(out=es[i][:, m, lo : lo + w], in_=ps[:, :w], func=FUNC.Tanh, bias=bu[:, m : m + 1])
+            t = STEPS[j][0]
+            w = width(j)
+            if m == 0:
+                es[j] = late.tile([P, NCH, W], F32, name="e")
+            ps = ps2.tile([P, W], F32, name="pz", tag="ps2")
+            mx(ps, w, "w2", 0, m, vcs[j][0], vcs[j][1], True, False)
+            mx(ps, w, "w3", 0, m, uq[t][:].rearrange("p k c -> p (k c)"), us[t][:].rearrange("p k c -> p (k c)"), False, True)
+            nc.scalar.activation(out=es[j][:, m, :w], in_=ps[:, :w], func=FUNC.Tanh, bias=bu[:, m : m + 1])
 
         def ex(j, m0, m1):
-            i, h = divmod(j, 2)
-            lo, w, pieces = HALVES[h]
-            part = es[i][:, m0:m1, lo : lo + w]
+            part = es[j][:, m0:m1, : width(j)]
             nc.scalar.activation(out=part, in_=part, func=FUNC.Exp)
 
         def prod(j, m0, m1):
-            i, h = divmod(j, 2)
-            lo, w, pieces = HALVES[h]
-            part = vis[i][:, m0:m1, lo : lo + w]
-            nc.vector.tensor_tensor(out=part, in0=es[i][:, m0:m1, lo : lo + w], in1=part, op=ALU.mult)
+            part = vis[j][:, m0:m1, : width(j)]
+            nc.vector.tensor_tensor(out=part, in0=es[j][:, m0:m1, : width(j)], in1=part, op=ALU.mult)
 
-        def tr(i, nd, lo, hi):
-            data = es[i] if nd == "den" else vis[i]
-            if lo == 0 and i < NT - 1:
-                pts[nd] = pst.tile([P, NCH, P], F32, name="pt", tag="pst")
-            elif lo == 0:
-                pts[nd] = ps1.tile([P, NCH, P], F32, name="pt", tag="ps1")
-            for k in range(lo, hi):
+        def tr(j, nd):
+            t, k0, nk = STEPS[j]
+            if t is None:
+                return
+            data = es[j] if nd == "den" else vis[j]
+            last_k = S // (P // TILES[t][1]) - 1
+            if k0 == 0:
+                pts[nd] = pst.tile([P, NCH, P], F32, name="pt_" + nd)
+            for k in range(nk):
                 for m in range(NCH):
                     nc.tensor.matmul(
                         pts[nd][:, m, :],
                         lhsT=data[:, m, k * P : (k + 1) * P],
                         rhs=ident32[:],
                         is_transpose=True,
-                        start=(k == 0 and m == 0),
-                        stop=(k == KK - 1 and m == NCH - 1),
+                        start=(k0 + k == 0 and m == 0),
+                        stop=(k0 + k == last_k and m == NCH - 1),
                     )
 
+        def ends(j):
+            t, k0, nk = STEPS[j]
+            return t is not None and (k0 + nk) * P // TILES[t][1] == S - 1
+
         def evac(nd, copy=nc.scalar.copy):
-            sjs[nd] = sjp.tile([P, NCH, P], F32, name="sj_" + nd)
+            sjs[nd] = sj[nd]
             copy(out=sjs[nd][:], in_=pts[nd][:])
 
         def back(nd):
-            pbs[nd] = pst.tile([P, NCH, P], F32, name="pb", tag="pst")
+            pbs[nd] = ps1.tile([P, NCH, P], F32, name="pb", tag="ps1")
             for m in range(NCH):
                 nc.tensor.transpose(pbs[nd][:, m, :], sjs[nd][:, m, :], ident32[:])
 
-        def red(i, nd):
+        def red(t, nd):
+            b0, nb = TILES[t]
             nc.vector.tensor_reduce(
-                out=sums[nd][:, :, TB * i : TB * (i + 1)],
-                in_=pbs[nd][:, :, 0 : TB * RUN].rearrange("p m (b r) -> p m b r", r=RUN),
+                out=sums[nd][:, :, b0 : b0 + nb],
+                in_=pbs[nd][:].rearrange("p m (b r) -> p m b r", b=nb),
                 axis=AXIS.X,
                 op=ALU.add,
             )
-            nc.vector.tensor_copy(out=tail[nd][:, :, :, i], in_=pbs[nd][:, :, TB * RUN : P])
 
-        def red_tail(nd):
-            nc.vector.tensor_reduce(out=sums[nd][:, :, TB * NT : B], in_=tail[nd][:], axis=AXIS.X, op=ALU.add)
+        def add_last(nd, lo, hi):
+            src = es[jl] if nd == "den" else vis[jl]
+            nc.vector.tensor_tensor(
+                out=sums[nd][:, :, lo:hi], in0=sums[nd][:, :, lo:hi], in1=src[:, :, lo:hi], op=ALU.add
+            )
 
         def recip(lo, hi):
             nc.vector.reciprocal(out=sums["den"][:, :, lo:hi], in_=sums["den"][:, :, lo:hi])
@@ -252,8 +264,8 @@ def tile_attentionmechanism_pa_t_kernel(tc, v_i, v_q, l1_w, l1_b, w_vi0, w_u0, b
                 wraw[nm] = early.tile([P, NCH, 512 * wpass[nm]], BF16, name=nm + "raw")
                 wgrp[nm] = early.tile([P, wpass[nm], NCH, P, 4], BF16, align_bytes=64, name=nm + "g")
             vqr = early.tile([P, T, HID], BF16, name="vqr")
-            ug = early.tile([P, B, 4], BF16, name="ug")
-            urep = early.tile([P, NT, P, 4], BF16, align_bytes=64, name="urep")
+            ug = early.tile([P, B, 4], BF16, align_bytes=64, name="ug")
+            urep = early.tile([P, len(TILES), P, 4], BF16, align_bytes=64, name="urep")
 
             def loadw(nm):
                 nc.sync.dma_start(out=wraw[nm][:], in_=wsrc[nm].rearrange("(j m) k -> j m k", m=NCH))
@@ -275,11 +287,7 @@ def tile_attentionmechanism_pa_t_kernel(tc, v_i, v_q, l1_w, l1_b, w_vi0, w_u0, b
                     )
 
             def wq(nm, g):
-                nc.vector.quantize_mx(
-                    out=wq_[nm][:, g, :].bitcast(FP8X4),
-                    scales=ws_[nm][:, g, :],
-                    in_=wgrp[nm][:, g].rearrange("p m j t -> p (m j t)"),
-                )
+                quant(wq_[nm][:, g, :], ws_[nm][:, g, :], wgrp[nm][:, g].rearrange("p m j t -> p (m j t)"))
 
             def uc(c):
                 if c == 0:
@@ -298,147 +306,143 @@ def tile_attentionmechanism_pa_t_kernel(tc, v_i, v_q, l1_w, l1_b, w_vi0, w_u0, b
             def ugr():
                 nc.vector.tensor_copy(out=ug[:], in_=pst_u["put"][:].rearrange("j m b -> j b m"))
 
-            def uqu(lo, hi, pieces):
-                n = hi - lo
+            def urp(t):
+                b0, nb = TILES[t]
                 nc.vector.tensor_copy(
-                    out=urep[:, lo:hi, 0 : TB * RUN, :].rearrange("p n (b r) t -> p n b r t", r=RUN),
-                    in_=ug[:, TB * lo : TB * hi, :]
-                    .rearrange("p (n b) t -> p n b t", n=n)
-                    .unsqueeze(3)
-                    .to_broadcast([P, n, TB, RUN, 4]),
+                    out=urep[:, t].rearrange("p (b r) t -> p b r t", b=nb),
+                    in_=ug[:, b0 : b0 + nb, :].unsqueeze(2).to_broadcast([P, nb, P // nb, 4]),
+                )
+
+            def uqu(t):
+                quant(uq[t][:, 0, :], us[t][:, 0, :], urep[:, t].rearrange("p c t -> p (c t)"))
+
+            def ufour(t):
+                nc.vector.tensor_copy(
+                    out=uq[t][:, 1:4, :].bitcast(I32), in_=uq[t][:, 0:1, :].bitcast(I32).to_broadcast([P, 3, P])
                 )
                 nc.vector.tensor_copy(
-                    out=urep[:, lo:hi, TB * RUN : P, :],
-                    in_=ug[:, TB * NT : B, :].unsqueeze(1).to_broadcast([P, n, 2, 4]),
-                )
-                quant(
-                    uq[:, lo * P : hi * P], us[:, lo * P : hi * P], urep[:, lo:hi].rearrange("p n c t -> p (n c) t"), pieces
+                    out=us[t][:, 1:4, :].bitcast(I32), in_=us[t][:, 0:1, :].bitcast(I32).to_broadcast([P, 3, P // 4])
                 )
 
             loadb()
             loadw("w1")
-            loadx()
             load(0)
             loadw("w3")
             loadw("w2")
             load(1)
             loadvq()
-            castb()
+            load(2)
+            load(3)
             wt("w1", 0)
             wt("w1", 1)
             rx(0, 0)
+            castb(l1b, l1b_raw)
             wq("w1", 0)
             wq("w1", 1)
-            qx(0, 0, 0)
-            qx(0, 1, 0)
-            rx_scalar(0, 1, range(4, KK))
-            rx(0, 1, ((0, 4),))
+            rx(0, 1)
             wt("w3", 0)
             wt("w2", 0)
-            qx(0, 0, 1)
-            qx(0, 1, 1)
-            for j in range(2):
-                for m in range(NCH):
-                    mm1(j, m)
             rx(1, 0)
-            v(0)
-            qv(0)
-            v(1)
-            qv(1)
-            qx(1, 0, 0)
-            qx(1, 1, 0)
-            rx_scalar(1, 1, range(KK))
-            rx(1, 1, ())
+            qx(0)
+            rx(1, 1)
+            for m in range(NCH):
+                mm1(0, m)
             wq("w3", 0)
+            qx(1)
+            for m in range(NCH):
+                mm1(1, m)
             wq("w2", 0)
+            castb(bu, bu_raw)
+            v(0)
+            rx(2, 0)
+            qv(0)
+            rx(2, 1)
+            v(1)
+            rx(3, 0)
+            qv(1)
+            rx(3, 1)
+            qx(2)
             for c in range(4):
                 uc(c)
             usc()
             ugr()
-            qx(1, 0, 1)
-            uqu(0, 1, ((0, 128),))
-            qx(1, 1, 1)
-            uqu(1, NT, ((0, 512), (512, 256)))
+            urp(0)
+            urp(1)
+            uqu(0)
+            ufour(0)
+            uqu(1)
+            ufour(1)
+            for t in range(2, len(TILES)):
+                urp(t)
+            for t in range(2, len(TILES)):
+                uqu(t)
+            for t in range(2, len(TILES)):
+                ufour(t)
+            quant(uq[None][:, 0, :], us[None][:, 0, :], ug[:].rearrange("p b t -> p (b t)"))
 
         late = ctx.enter_context(tc.tile_pool(name="late", bufs=3))
-        nb = 2 * NT
-        last = NT - 1
-        for j in range(nb):
-            i, h = divmod(j, 2)
-            nd = "num" if h else "den"
-            other = "den" if h else "num"
-            front = j + 2 < nb
-            if h == 0 and i + 2 < NT:
-                load(i + 2)
-            if 0 < j < nb - 1:
+        lo_b = TILES[-1][0]
+        for j in range(ns):
+            if j in (0, 2):
+                load(4 + j)
+                load(5 + j)
+            if 0 < j < ns - 1:
                 v(j + 1)
-            if i + 2 < NT:
-                if h == 0:
-                    rx(i + 2, 0)
-                else:
-                    qx(i + 2, 0, 0)
-                    qx(i + 2, 0, 1)
-            if 0 < j < nb - 1:
+            if j + 4 < ns and j + 4 != jl:
+                rx(j + 4, 0)
+            if 0 < j < ns - 1:
                 qv(j + 1)
-            if i + 2 < NT:
-                if h == 0:
-                    rx(i + 2, 1)
-                else:
-                    qx(i + 2, 1, 0)
-                    qx(i + 2, 1, 1)
-            if nb - 4 <= j < nb - 2:
-                recip(2 * TB * (j - nb + 4), 2 * TB * (j - nb + 5))
-            if j == nb - 2:
-                recip(TB * (last - 2), TB * (last - 1))
+            if j + 4 < ns and j + 4 != jl:
+                rx(j + 4, 1)
+            if j + 3 < ns:
+                qx(j + 3)
             if j >= 1:
-                prod(j - 1, 0, 4)
-            if front:
+                prod(j - 1, 0, NCH)
+            if j + 2 < ns:
                 mm1(j + 2, 0)
                 mm1(j + 2, 1)
-                if i >= 1:
-                    tr(i - 1, nd, 0, 4)
                 for m in range(2):
-                    mm1(j + 2, 2 + m)
                     mm2(j, m)
+                    mm1(j + 2, 2 + m)
+                mm2(j, 2)
+                mm2(j, 3)
             else:
                 for m in range(NCH):
                     mm2(j, m)
-                if j < nb - 1:
-                    ex(j, 0, 4)
-                tr(i - 1, nd, 0, 4)
-            if i >= 1 + (1 - h):
-                back(other)
-                red(i - 2 + h, other)
-            if i >= 1:
-                tr(i - 1, nd, 4, KK)
-            if front:
-                for m in range(2, 4):
-                    mm2(j, m)
-                if i >= 1:
-                    evac(nd)
-                ex(j, 0, 4)
-            elif j < nb - 1:
-                evac(nd, nc.vector.tensor_copy)
-        recip(TB * (last - 1), TB * last)
-        evac("num", nc.vector.tensor_copy)
+            if j < ns - 1:
+                ex(j, 0, NCH)
+            if j >= 3 and ends(j - 3):
+                back("num")
+                red(STEPS[j - 3][0], "num")
+            if j >= 2 and ends(j - 2):
+                back("den")
+                red(STEPS[j - 2][0], "den")
+            if j >= 2:
+                tr(j - 2, "num")
+            if j >= 1:
+                tr(j - 1, "den")
+            if j >= 2 and ends(j - 2):
+                evac("num")
+            if j >= 1 and ends(j - 1):
+                evac("den")
+        add_last("den", 0, lo_b)
+        recip(0, lo_b)
         for m in range(NCH):
-            ex(nb - 1, m, m + 1)
-            prod(nb - 1, m, m + 1)
-        tr(last, "den", 0, 4)
-        back("num")
-        red(last - 1, "num")
-        tr(last, "num", 0, 4)
-        tr(last, "den", 4, KK)
+            ex(ns - 1, m, m + 1)
+            prod(ns - 1, m, m + 1)
+        tr(ns - 2, "num")
+        tr(ns - 1, "den")
         evac("den")
-        tr(last, "num", 4, KK)
+        tr(ns - 1, "num")
         evac("num", nc.vector.tensor_copy)
         back("den")
         back("num")
-        ratio(0, TB * last)
-        red(last, "den")
-        red_tail("den")
-        recip(TB * last, B)
-        red(last, "num")
-        red_tail("num")
-        ratio(TB * last, B)
+        add_last("num", 0, lo_b)
+        ratio(0, lo_b)
+        red(len(TILES) - 1, "den")
+        add_last("den", lo_b, B)
+        recip(lo_b, B)
+        red(len(TILES) - 1, "num")
+        add_last("num", lo_b, B)
+        ratio(lo_b, B)
         finish()

@@ -69,6 +69,8 @@ def tile_attentionmechanism_pa_t_kernel(tc, v_i, v_q, l1_w, l1_b, w_vi0, w_u0, b
         us[None] = keep.tile([P, 1, P], U8, align_bytes=64, name="usl")
         sums = {nd: keep.tile([P, NCH, B], F32, name="sum_" + nd) for nd in ("num", "den")}
         sj = {nd: keep.tile([P, NCH, P], F32, name="sj_" + nd) for nd in ("num", "den")}
+        ug = keep.tile([P, B, 4], BF16, align_bytes=64, name="ug")
+        urep = keep.tile([P, len(TILES), P, 4], BF16, align_bytes=64, name="urep")
         osb = keep.tile([P, P, NCH], F32, name="osb")
         for t in range(len(TILES)):
             nc.gpsimd.memset(us[t][:, 0, :].bitcast(I32), 0)
@@ -89,10 +91,10 @@ def tile_attentionmechanism_pa_t_kernel(tc, v_i, v_q, l1_w, l1_b, w_vi0, w_u0, b
             return STEPS[j][2] * P
 
         def load(c):
-            raws[c] = [rawp.tile([P, CH, ROW], BF16, name="raw%d" % g) for g in range(2)]
+            raws[c] = rawp.tile([P, 2, CH, ROW], BF16, name="raw")
             for g in range(2):
                 nc.sync.dma_start(
-                    out=raws[c][g][:, :, : 4 * S],
+                    out=raws[c][:, g, :, : 4 * S],
                     in_=v_i[CH * c : CH * (c + 1), g * 512 : (g + 1) * 512].rearrange("b (p t) h w -> p b (t h w)", t=4),
                 )
 
@@ -111,13 +113,17 @@ def tile_attentionmechanism_pa_t_kernel(tc, v_i, v_q, l1_w, l1_b, w_vi0, w_u0, b
                 xgs[j] = xgp.tile([P, 2, W, 4], BF16, align_bytes=64, name="xg")
             dst = xgs[j][:, g, : nk * P, :].rearrange("p (k b r) t -> p k b t r", k=nk, r=r)
             for c in range(b0 // CH, (b0 + nb) // CH):
-                src = raws[c][g][:, :, : 4 * S].rearrange("p b (t s) -> p b t s", t=4)
+                src = raws[c][:, g, :, : 4 * S].rearrange("p b (t s) -> p b t s", t=4)
                 nc.vector.tensor_copy(
                     out=dst[:, :, c * CH - b0 : (c + 1) * CH - b0],
                     in_=src[:, :, :, k0 * r : (k0 + nk) * r].rearrange("p b t (k r) -> p k b t r", r=r),
                 )
-                if k0 == 0:
-                    nc.vector.tensor_copy(out=xl[:, g, CH * c : CH * (c + 1), :], in_=src[:, :, :, S - 1])
+
+        def rx_last(c):
+            nc.scalar.copy(
+                out=xl[:, :, CH * c : CH * (c + 1), :],
+                in_=raws[c][:, :, :, : 4 * S].rearrange("p g b (t s) -> p g b t s", t=4)[:, :, :, :, S - 1],
+            )
 
         def quant(codes, scales, src):
             nc.vector.quantize_mx(out=codes.bitcast(FP8X4), scales=scales, in_=src)
@@ -190,7 +196,7 @@ def tile_attentionmechanism_pa_t_kernel(tc, v_i, v_q, l1_w, l1_b, w_vi0, w_u0, b
             part = vis[j][:, m0:m1, : width(j)]
             nc.vector.tensor_tensor(out=part, in0=es[j][:, m0:m1, : width(j)], in1=part, op=ALU.mult)
 
-        def tr(j, nd):
+        def tr(j, nd, m0=0, m1=NCH):
             t, k0, nk = STEPS[j]
             if t is None:
                 return
@@ -199,7 +205,7 @@ def tile_attentionmechanism_pa_t_kernel(tc, v_i, v_q, l1_w, l1_b, w_vi0, w_u0, b
             if k0 == 0:
                 pts[nd] = pst.tile([P, NCH, P], F32, name="pt_" + nd)
             for k in range(nk):
-                for m in range(NCH):
+                for m in range(m0, m1):
                     nc.tensor.matmul(
                         pts[nd][:, m, :],
                         lhsT=data[:, m, k * P : (k + 1) * P],
@@ -264,8 +270,6 @@ def tile_attentionmechanism_pa_t_kernel(tc, v_i, v_q, l1_w, l1_b, w_vi0, w_u0, b
                 wraw[nm] = early.tile([P, NCH, 512 * wpass[nm]], BF16, name=nm + "raw")
                 wgrp[nm] = early.tile([P, wpass[nm], NCH, P, 4], BF16, align_bytes=64, name=nm + "g")
             vqr = early.tile([P, T, HID], BF16, name="vqr")
-            ug = early.tile([P, B, 4], BF16, align_bytes=64, name="ug")
-            urep = early.tile([P, len(TILES), P, 4], BF16, align_bytes=64, name="urep")
 
             def loadw(nm):
                 nc.sync.dma_start(out=wraw[nm][:], in_=wsrc[nm].rearrange("(j m) k -> j m k", m=NCH))
@@ -304,7 +308,7 @@ def tile_attentionmechanism_pa_t_kernel(tc, v_i, v_q, l1_w, l1_b, w_vi0, w_u0, b
                     nc.tensor.transpose(pst_u["put"][:, m, :], u32[:, m, :], ident32[:])
 
             def ugr():
-                nc.vector.tensor_copy(out=ug[:], in_=pst_u["put"][:].rearrange("j m b -> j b m"))
+                nc.scalar.copy(out=ug[:], in_=pst_u["put"][:].rearrange("j m b -> j b m"))
 
             def urp(t):
                 b0, nb = TILES[t]
@@ -362,6 +366,8 @@ def tile_attentionmechanism_pa_t_kernel(tc, v_i, v_q, l1_w, l1_b, w_vi0, w_u0, b
             qv(1)
             rx(3, 1)
             qx(2)
+            rx_last(0)
+            rx_last(1)
             for c in range(4):
                 uc(c)
             usc()
@@ -398,6 +404,9 @@ def tile_attentionmechanism_pa_t_kernel(tc, v_i, v_q, l1_w, l1_b, w_vi0, w_u0, b
                 qx(j + 3)
             if j >= 1:
                 prod(j - 1, 0, NCH)
+            if j == ns - 2:
+                add_last("den", 0, lo_b)
+                recip(0, lo_b)
             if j + 2 < ns:
                 mm1(j + 2, 0)
                 mm1(j + 2, 1)
@@ -411,6 +420,9 @@ def tile_attentionmechanism_pa_t_kernel(tc, v_i, v_q, l1_w, l1_b, w_vi0, w_u0, b
                     mm2(j, m)
             if j < ns - 1:
                 ex(j, 0, NCH)
+            if j in (1, 4, 7):
+                for c in range(2 * (j + 2) // 3, 2 * (j + 2) // 3 + 2):
+                    rx_last(c)
             if j >= 3 and ends(j - 3):
                 back("num")
                 red(STEPS[j - 3][0], "num")
@@ -425,20 +437,19 @@ def tile_attentionmechanism_pa_t_kernel(tc, v_i, v_q, l1_w, l1_b, w_vi0, w_u0, b
                 evac("num")
             if j >= 1 and ends(j - 1):
                 evac("den")
-        add_last("den", 0, lo_b)
-        recip(0, lo_b)
+        add_last("num", 0, lo_b)
         for m in range(NCH):
             ex(ns - 1, m, m + 1)
             prod(ns - 1, m, m + 1)
+        ratio(0, lo_b)
         tr(ns - 2, "num")
-        tr(ns - 1, "den")
+        for m in (0, 2):
+            tr(ns - 1, "den", m, m + 2)
+            tr(ns - 1, "num", m, m + 2)
         evac("den")
-        tr(ns - 1, "num")
         evac("num", nc.vector.tensor_copy)
         back("den")
         back("num")
-        add_last("num", 0, lo_b)
-        ratio(0, lo_b)
         red(len(TILES) - 1, "den")
         add_last("den", lo_b, B)
         recip(lo_b, B)

from contextlib import ExitStack

import concourse.mybir as mybir
from concourse.masks import make_identity

F32 = mybir.dt.float32
BF16 = mybir.dt.bfloat16
U32 = mybir.dt.uint32
I32 = mybir.dt.int32
U8 = mybir.dt.uint8
FP8X4 = mybir.dt.float8_e4m3fn_x4
FUNC = mybir.ActivationFunctionType
ALU = mybir.AluOpType
AXIS = mybir.AxisListType

B, C, S, T, HID = 128, 1024, 49, 20, 512
P = 128
NCH = 4
W = 512
ROW = 208
CH = 16
TILES = ((0, 16), (16, 16), (32, 32), (64, 32), (96, 32))
STEPS = (
    [(t, k, n) for t in (0, 1) for k, n in ((0, 4), (4, 2))]
    + [(t, k, 4) for t in (2, 3) for k in (0, 4, 8)]
    + [(4, 0, 4), (None, 0, 1), (4, 4, 4), (4, 8, 4)]
)
FLOPS = 2 * B * S * C * HID + 2 * B * S * HID * HID + 2 * B * HID * HID


def tile_attentionmechanism_pa_t_kernel(tc, v_i, v_q, l1_w, l1_b, w_vi0, w_u0, b_u0, out):
    nc = tc.nc
    ns = len(STEPS)
    jl = STEPS.index((None, 0, 1))

    with ExitStack() as ctx:
        keep = ctx.enter_context(tc.tile_pool(name="keep", bufs=1))
        rawp = ctx.enter_context(tc.tile_pool(name="rawp", bufs=4))
        xgp = ctx.enter_context(tc.tile_pool(name="xgp", bufs=3))
        two = ctx.enter_context(tc.tile_pool(name="two", bufs=2))
        vip = ctx.enter_context(tc.tile_pool(name="vip", bufs=5))
        ps1 = ctx.enter_context(tc.psum_pool(name="ps1", bufs=3))
        ps2 = ctx.enter_context(tc.psum_pool(name="ps2", bufs=3))
        pst = ctx.enter_context(tc.psum_pool(name="pst", bufs=1))
        ctx.enter_context(tc.manual_schedule())

        xl = keep.tile([P, 2, P, 4], BF16, align_bytes=64, name="xl")

        ident32 = keep.tile([P, P], F32, name="ident32")
        make_identity(nc, ident32[:])
        identb = keep.tile([P, P], BF16, name="identb")
        make_identity(nc, identb[:])

        wsrc = {"w1": l1_w, "w2": w_vi0, "w3": w_u0}
        wpass = {"w1": 2, "w2": 1, "w3": 1}
        wq_ = {}
        ws_ = {}
        for nm in ("w1", "w2", "w3"):
            wq_[nm] = keep.tile([P, wpass[nm], NCH * P], U32, align_bytes=64, name=nm + "q")
            ws_[nm] = keep.tile([P, wpass[nm], NCH * P], U8, align_bytes=64, name=nm + "s")
        l1b_raw = keep.tile([P, NCH], BF16, name="l1b_raw")
        bu_raw = keep.tile([P, NCH], BF16, name="bu_raw")
        l1b = keep.tile([P, NCH], F32, name="l1b")
        bu = keep.tile([P, NCH], F32, name="bu")
        u32 = keep.tile([P, NCH, P], F32, name="u32")
        uq = {t: keep.tile([P, 4, P], U32, align_bytes=64, name="uq%d" % t) for t in range(len(TILES))}
        us = {t: keep.tile([P, 4, P], U8, align_bytes=64, name="us%d" % t) for t in range(len(TILES))}
        uq[None] = keep.tile([P, 1, P], U32, align_bytes=64, name="uql")
        us[None] = keep.tile([P, 1, P], U8, align_bytes=64, name="usl")
        sums = {nd: keep.tile([P, NCH, B], F32, name="sum_" + nd) for nd in ("num", "den")}
        sj = {nd: keep.tile([P, NCH, P], F32, name="sj_" + nd) for nd in ("num", "den")}
        ug = keep.tile([P, B, 4], BF16, align_bytes=64, name="ug")
        urep = keep.tile([P, len(TILES), P, 4], BF16, align_bytes=64, name="urep")
        osb = keep.tile([P, P, NCH], F32, name="osb")
        for t in range(len(TILES)):
            nc.gpsimd.memset(us[t][:, 0, :].bitcast(I32), 0)

        raws = {}
        xgs = {}
        xqs = {}
        vgs = {}
        vcs = {}
        vis = {}
        es = {}
        pts = {}
        sjs = {}
        pbs = {}
        pst_u = {}

        def width(j):
            return STEPS[j][2] * P

        def load(c):
            raws[c] = rawp.tile([P, 2, CH, ROW], BF16, name="raw")
            for g in range(2):
                nc.sync.dma_start(
                    out=raws[c][:, g, :, : 4 * S],
                    in_=v_i[CH * c : CH * (c + 1), g * 512 : (g + 1) * 512].rearrange("b (p t) h w -> p b (t h w)", t=4),
                )

        def loadb():
            nc.scalar.dma_start(out=l1b_raw[:], in_=l1_b.rearrange("(j m) -> j m", m=NCH))
            nc.scalar.dma_start(out=bu_raw[:], in_=b_u0.rearrange("(j m) -> j m", m=NCH))

        def castb(dst, src):
            nc.vector.tensor_copy(out=dst[:], in_=src[:])

        def rx(j, g):
            t, k0, nk = STEPS[j]
            b0, nb = TILES[t]
            r = P // nb
            if g == 0:
                xgs[j] = xgp.tile([P, 2, W, 4], BF16, align_bytes=64, name="xg")
            dst = xgs[j][:, g, : nk * P, :].rearrange("p (k b r) t -> p k b t r", k=nk, r=r)
            for c in range(b0 // CH, (b0 + nb) // CH):
                src = raws[c][:, g, :, : 4 * S].rearrange("p b (t s) -> p b t s", t=4)
                nc.vector.tensor_copy(
                    out=dst[:, :, c * CH - b0 : (c + 1) * CH - b0],
                    in_=src[:, :, :, k0 * r : (k0 + nk) * r].rearrange("p b t (k r) -> p k b t r", r=r),
                )

        def rx_last(c):
            nc.scalar.copy(
                out=xl[:, :, CH * c : CH * (c + 1), :],
                in_=raws[c][:, :, :, : 4 * S].rearrange("p g b (t s) -> p g b t s", t=4)[:, :, :, :, S - 1],
            )

        def quant(codes, scales, src):
            nc.vector.quantize_mx(out=codes.bitcast(FP8X4), scales=scales, in_=src)

        def qx(j):
            w = width(j)
            xqs[j] = (
                two.tile([P, 2, W], U32, align_bytes=64, name="xq"),
                two.tile([P, 2, W], U8, align_bytes=64, name="xs"),
            )
            src = xl if STEPS[j][0] is None else xgs[j]
            if w == W:
                quant(
                    xqs[j][0][:].rearrange("p g c -> p (g c)"),
                    xqs[j][1][:].rearrange("p g c -> p (g c)"),
                    src[:].rearrange("p g c t -> p (g c t)"),
                )
            else:
                for g in range(2):
                    quant(xqs[j][0][:, g, :w], xqs[j][1][:, g, :w], src[:, g, :w, :].rearrange("p c t -> p (c t)"))

        def mx(ps, n, w, g, m, codes, scales, start, stop):
            nc.tensor.matmul_mx(
                out=ps[:, :n],
                lhsT=wq_[w][:, g, m * P : (m + 1) * P].bitcast(FP8X4),
                lhsT_scale=ws_[w][:, g, m * P : (m + 1) * P],
                rhs=codes[:, :n].bitcast(FP8X4),
                rhs_scale=scales[:, :n],
                start=start,
                stop=stop,
            )

        def mm1(j, m):
            w = width(j)
            if m == 0:
                vis[j] = vip.tile([P, NCH, W], F32, name="vi")
            ps = ps1.tile([P, W], F32, name="ps", tag="ps1")
            for g in range(2):
                mx(ps, w, "w1", g, m, xqs[j][0][:, g], xqs[j][1][:, g], g == 0, g == 1)
            nc.scalar.activation(out=vis[j][:, m, :w], in_=ps[:, :w], func=FUNC.Tanh, bias=l1b[:, m : m + 1])

        def v(j):
            w = width(j)
            vgs[j] = two.tile([P, W, 4], BF16, align_bytes=64, name="vg")
            nc.vector.tensor_copy(out=vgs[j][:, :w, :], in_=vis[j][:, :, :w].rearrange("p m c -> p c m"))

        def qv(j):
            w = width(j)
            vcs[j] = (
                two.tile([P, W], U32, align_bytes=64, name="vc"),
                two.tile([P, W], U8, align_bytes=64, name="vs"),
            )
            quant(vcs[j][0][:, :w], vcs[j][1][:, :w], vgs[j][:, :w, :].rearrange("p c t -> p (c t)"))

        def mm2(j, m):
            t = STEPS[j][0]
            w = width(j)
            if m == 0:
                es[j] = late.tile([P, NCH, W], F32, name="e")
            ps = ps2.tile([P, W], F32, name="pz", tag="ps2")
            mx(ps, w, "w2", 0, m, vcs[j][0], vcs[j][1], True, False)
            mx(ps, w, "w3", 0, m, uq[t][:].rearrange("p k c -> p (k c)"), us[t][:].rearrange("p k c -> p (k c)"), False, True)
            nc.scalar.activation(out=es[j][:, m, :w], in_=ps[:, :w], func=FUNC.Tanh, bias=bu[:, m : m + 1])

        def ex(j, m0, m1):
            part = es[j][:, m0:m1, : width(j)]
            nc.scalar.activation(out=part, in_=part, func=FUNC.Exp)

        def prod(j, m0, m1):
            part = vis[j][:, m0:m1, : width(j)]
            nc.vector.tensor_tensor(out=part, in0=es[j][:, m0:m1, : width(j)], in1=part, op=ALU.mult)

        def tr(j, nd, m0=0, m1=NCH):
            t, k0, nk = STEPS[j]
            if t is None:
                return
            data = es[j] if nd == "den" else vis[j]
            last_k = S // (P // TILES[t][1]) - 1
            if k0 == 0:
                pts[nd] = pst.tile([P, NCH, P], F32, name="pt_" + nd)
            for k in range(nk):
                for m in range(m0, m1):
                    nc.tensor.matmul(
                        pts[nd][:, m, :],
                        lhsT=data[:, m, k * P : (k + 1) * P],
                        rhs=ident32[:],
                        is_transpose=True,
                        start=(k0 + k == 0 and m == 0),
                        stop=(k0 + k == last_k and m == NCH - 1),
                    )

        def ends(j):
            t, k0, nk = STEPS[j]
            return t is not None and (k0 + nk) * P // TILES[t][1] == S - 1

        def evac(nd, copy=nc.scalar.copy):
            sjs[nd] = sj[nd]
            copy(out=sjs[nd][:], in_=pts[nd][:])

        def back(nd):
            pbs[nd] = ps1.tile([P, NCH, P], F32, name="pb", tag="ps1")
            for m in range(NCH):
                nc.tensor.transpose(pbs[nd][:, m, :], sjs[nd][:, m, :], ident32[:])

        def red(t, nd):
            b0, nb = TILES[t]
            nc.vector.tensor_reduce(
                out=sums[nd][:, :, b0 : b0 + nb],
                in_=pbs[nd][:].rearrange("p m (b r) -> p m b r", b=nb),
                axis=AXIS.X,
                op=ALU.add,
            )

        def add_last(nd, lo, hi):
            src = es[jl] if nd == "den" else vis[jl]
            nc.vector.tensor_tensor(
                out=sums[nd][:, :, lo:hi], in0=sums[nd][:, :, lo:hi], in1=src[:, :, lo:hi], op=ALU.add
            )

        def recip(lo, hi):
            nc.vector.reciprocal(out=sums["den"][:, :, lo:hi], in_=sums["den"][:, :, lo:hi])

        def ratio(lo, hi):
            nc.vector.tensor_tensor(
                out=sums["num"][:, :, lo:hi], in0=sums["num"][:, :, lo:hi], in1=sums["den"][:, :, lo:hi], op=ALU.mult
            )

        def finish():
            po = ps1.tile([P, NCH, P], F32, name="po", tag="ps1")
            for m in range(NCH):
                nc.tensor.transpose(po[:, m, :], sums["num"][:, m, :], ident32[:])
            nc.vector.tensor_tensor(
                out=osb[:],
                in0=po[:].rearrange("b m j -> b j m"),
                in1=u32[:].rearrange("b m j -> b j m"),
                op=ALU.add,
            )
            nc.sync.dma_start(out=out[:, :], in_=osb[:].rearrange("b j m -> b (j m)"))

        with tc.tile_pool(name="early", bufs=1) as early:
            wraw = {}
            wgrp = {}
            for nm in ("w1", "w2", "w3"):
                wraw[nm] = early.tile([P, NCH, 512 * wpass[nm]], BF16, name=nm + "raw")
                wgrp[nm] = early.tile([P, wpass[nm], NCH, P, 4], BF16, align_bytes=64, name=nm + "g")
            vqr = early.tile([P, T, HID], BF16, name="vqr")

            def loadw(nm):
                nc.sync.dma_start(out=wraw[nm][:], in_=wsrc[nm].rearrange("(j m) k -> j m k", m=NCH))

            def loadvq():
                for c in range(4):
                    nc.sync.dma_start(out=vqr[:, 5 * c : 5 * c + 5, :], in_=v_q[:, 5 * c : 5 * c + 5, :])

            def wt(nm, g):
                for mh in range(2):
                    pt = ps1.tile([P, 2, 2, P], F32, name="pw", tag="ps1")
                    for mm in range(2):
                        words = wraw[nm][:, 2 * mh + mm, :].bitcast(F32).rearrange("p (g q u) -> p g u q", g=wpass[nm], u=2)
                        for u in range(2):
                            nc.tensor.transpose(pt[:, mm, u, :], words[:, g, u, :], ident32[:])
                    nc.scalar.copy(
                        out=wgrp[nm][:, g, 2 * mh : 2 * mh + 2, :, :].bitcast(F32),
                        in_=pt[:].rearrange("p a u j -> p a j u"),
                    )

            def wq(nm, g):
                quant(wq_[nm][:, g, :], ws_[nm][:, g, :], wgrp[nm][:, g].rearrange("p m j t -> p (m j t)"))

            def uc(c):
                if c == 0:
                    pst_u["pu"] = ps2.tile([P, HID], F32, name="pu", tag="ps2")
                for t in range(5 * c, 5 * c + 5):
                    nc.tensor.matmul(pst_u["pu"][:], lhsT=identb[:], rhs=vqr[:, t, :], start=(t == 0), stop=(t == T - 1))

            def usc():
                nc.scalar.activation(
                    out=u32[:], in_=pst_u["pu"][:].rearrange("b (j m) -> b m j", m=NCH), func=FUNC.Copy, scale=1.0 / T
                )
                pst_u["put"] = ps2.tile([P, NCH, P], F32, name="put", tag="ps2")
                for m in range(NCH):
                    nc.tensor.transpose(pst_u["put"][:, m, :], u32[:, m, :], ident32[:])

            def ugr():
                nc.scalar.copy(out=ug[:], in_=pst_u["put"][:].rearrange("j m b -> j b m"))

            def urp(t):
                b0, nb = TILES[t]
                nc.vector.tensor_copy(
                    out=urep[:, t].rearrange("p (b r) t -> p b r t", b=nb),
                    in_=ug[:, b0 : b0 + nb, :].unsqueeze(2).to_broadcast([P, nb, P // nb, 4]),
                )

            def uqu(t):
                quant(uq[t][:, 0, :], us[t][:, 0, :], urep[:, t].rearrange("p c t -> p (c t)"))

            def ufour(t):
                nc.vector.tensor_copy(
                    out=uq[t][:, 1:4, :].bitcast(I32), in_=uq[t][:, 0:1, :].bitcast(I32).to_broadcast([P, 3, P])
                )
                nc.vector.tensor_copy(
                    out=us[t][:, 1:4, :].bitcast(I32), in_=us[t][:, 0:1, :].bitcast(I32).to_broadcast([P, 3, P // 4])
                )

            loadb()
            loadw("w1")
            load(0)
            loadw("w3")
            loadw("w2")
            load(1)
            loadvq()
            load(2)
            load(3)
            wt("w1", 0)
            wt("w1", 1)
            rx(0, 0)
            castb(l1b, l1b_raw)
            wq("w1", 0)
            wq("w1", 1)
            rx(0, 1)
            wt("w3", 0)
            wt("w2", 0)
            rx(1, 0)
            qx(0)
            rx(1, 1)
            for m in range(NCH):
                mm1(0, m)
            wq("w3", 0)
            qx(1)
            for m in range(NCH):
                mm1(1, m)
            wq("w2", 0)
            castb(bu, bu_raw)
            v(0)
            rx(2, 0)
            qv(0)
            rx(2, 1)
            v(1)
            rx(3, 0)
            qv(1)
            rx(3, 1)
            qx(2)
            rx_last(0)
            rx_last(1)
            for c in range(4):
                uc(c)
            usc()
            ugr()
            urp(0)
            urp(1)
            uqu(0)
            ufour(0)
            uqu(1)
            ufour(1)
            for t in range(2, len(TILES)):
                urp(t)
            for t in range(2, len(TILES)):
                uqu(t)
            for t in range(2, len(TILES)):
                ufour(t)
            quant(uq[None][:, 0, :], us[None][:, 0, :], ug[:].rearrange("p b t -> p (b t)"))

        late = ctx.enter_context(tc.tile_pool(name="late", bufs=3))
        lo_b = TILES[-1][0]
        for j in range(ns):
            if j in (0, 2):
                load(4 + j)
                load(5 + j)
            if 0 < j < ns - 1:
                v(j + 1)
            if j + 4 < ns and j + 4 != jl:
                rx(j + 4, 0)
            if 0 < j < ns - 1:
                qv(j + 1)
            if j + 4 < ns and j + 4 != jl:
                rx(j + 4, 1)
            if j + 3 < ns:
                qx(j + 3)
            if j >= 1:
                prod(j - 1, 0, NCH)
            if j == ns - 2:
                add_last("den", 0, lo_b)
                recip(0, lo_b)
            if j + 2 < ns:
                mm1(j + 2, 0)
                mm1(j + 2, 1)
                for m in range(2):
                    mm2(j, m)
                    mm1(j + 2, 2 + m)
                mm2(j, 2)
                mm2(j, 3)
            else:
                for m in range(NCH):
                    mm2(j, m)
            if j < ns - 1:
                ex(j, 0, NCH)
            if j in (1, 4, 7):
                for c in range(2 * (j + 2) // 3, 2 * (j + 2) // 3 + 2):
                    rx_last(c)
            if j >= 3 and ends(j - 3):
                back("num")
                red(STEPS[j - 3][0], "num")
            if j >= 2 and ends(j - 2):
                back("den")
                red(STEPS[j - 2][0], "den")
            if j >= 2:
                tr(j - 2, "num")
            if j >= 1:
                tr(j - 1, "den")
            if j >= 2 and ends(j - 2):
                evac("num")
            if j >= 1 and ends(j - 1):
                evac("den")
        add_last("num", 0, lo_b)
        for m in range(NCH):
            ex(ns - 1, m, m + 1)
            prod(ns - 1, m, m + 1)
        ratio(0, lo_b)
        tr(ns - 2, "num")
        for m in (0, 2):
            tr(ns - 1, "den", m, m + 2)
            tr(ns - 1, "num", m, m + 2)
        evac("den")
        evac("num", nc.vector.tensor_copy)
        back("den")
        back("num")
        red(len(TILES) - 1, "den")
        add_last("den", lo_b, B)
        recip(lo_b, B)
        red(len(TILES) - 1, "num")
        add_last("num", lo_b, B)
        ratio(lo_b, B)
        finish()
